import numpy as np
import ml_dtypes


def mxq(x, axis, fmt="e4m3"):
    dtype, down = {"e4m3": (ml_dtypes.float8_e4m3fn, 7), "e5m2": (ml_dtypes.float8_e5m2, 14)}[fmt]
    v = np.moveaxis(np.asarray(x, np.float32).astype(ml_dtypes.bfloat16).astype(np.float64), axis, -1)
    blocks = v.reshape(v.shape[:-1] + (-1, 32))
    amax = np.abs(blocks).max(-1, keepdims=True)
    byte = np.maximum(np.where(amax > 0, np.frexp(amax)[1] - 1 + 127, 0) - down, 1)
    scale = np.exp2(byte - 127.0)
    codes = (blocks / scale).astype(np.float32).astype(dtype).astype(np.float64)
    return np.moveaxis((codes * scale).reshape(v.shape), -1, axis)


WIDE = False


def mx_kscale(k):
    if not WIDE:
        return np.ones(k)
    levels = np.array([10, -10, 5, -5, 0])
    a = np.random.permutation(np.resize(levels, k // 512 * 4)).reshape(k // 512, 4)
    idx = np.arange(k)
    return np.exp2(a[idx // 512, idx % 128 // 32])


BF16 = ml_dtypes.bfloat16


def bf(x):
    return np.asarray(x, np.float32).astype(BF16)


def f64(x):
    return np.asarray(x).astype(np.float64)


E2M1 = np.array([0.0, 0.5, 1.0, 1.5, 2.0, 3.0, 4.0, 6.0, -0.0, -0.5, -1.0, -1.5, -2.0, -3.0, -4.0, -6.0])


def pack_weight(w, fmt):
    k, n = w.shape
    w = f64(bf(w)).reshape(k // 32, 32, n)
    amax = np.abs(w).max(1)
    if fmt == "e4m3":
        byte = np.frexp(amax)[1] - 1 + 127 - 7
    else:
        mant, ex = np.frexp(amax / 6.0)
        byte = np.where(mant > 0.5, ex, ex - 1) + 127
    byte = np.clip(np.where(amax > 0, byte, 1), 1, 254)
    scaled = (w * np.exp2(127.0 - byte)[:, None, :]).reshape(k, n).astype(np.float32)
    by_word = np.ascontiguousarray(scaled.reshape(k // 512, 128, 4, n).transpose(0, 1, 3, 2))
    if fmt == "e4m3":
        words = by_word.astype(ml_dtypes.float8_e4m3fn).view(np.uint8)
    else:
        c = by_word.astype(ml_dtypes.float4_e2m1fn).view(np.uint8) & 0xF
        words = c[..., 0::2] | (c[..., 1::2] << 4)
    return np.ascontiguousarray(words), np.ascontiguousarray(byte.astype(np.uint8).reshape(k // 512, 16, n))


def unpack_weight(words, scales, fmt):
    g, p, n, _ = words.shape
    if fmt == "e4m3":
        vals = np.ascontiguousarray(words).view(ml_dtypes.float8_e4m3fn).astype(np.float64)
    else:
        nib = np.empty((g, p, n, 4), np.uint8)
        nib[..., 0::2] = words & 0xF
        nib[..., 1::2] = words >> 4
        vals = E2M1[nib]
    vals = vals * np.repeat(np.exp2(scales.astype(np.float64) - 127.0), 8, axis=1)[..., None]
    return vals.transpose(0, 1, 3, 2).reshape(g * 512, n)

def pack4(w):
    words, scales = pack_weight(w, "e2m1")
    return words.reshape(words.shape[0], 128, -1), scales


def unpack4(words, scales):
    return unpack_weight(words.reshape(words.shape[0], 128, -1, 2), scales, "e2m1")


B, S, D = 32, 256, 512
NB = 2
W = 2 * NB + 1


def setup_inputs():
    s = mx_kscale(D)
    x = bf(np.random.standard_normal((B, S, D)) * s)
    wq = np.random.standard_normal((D, D)) / np.sqrt(D) / s[None, :]
    Wq_words, Wq_scales = pack4(wq.T)
    bq = bf(np.random.standard_normal(D) * 0.3)
    k_proj = bf(np.random.standard_normal((B, S, D)))
    return {"x": x,
            "Wq_words": Wq_words,
            "Wq_scales": Wq_scales,
            "bq": bq,
            "k_proj": k_proj}


def reference(x, Wq_words, Wq_scales, bq, k_proj):
    kf = f64(k_proj)
    q = (mxq(f64(x), 2, "e4m3") @ unpack4(Wq_words, Wq_scales)) + f64(bq)
    scores = np.full((B, S, W), -np.inf)
    for j in range(W):
        o = j - NB
        lo, hi = max(0, -o), S - max(0, o)
        scores[:, lo:hi, j] = (q[:, lo:hi] * kf[:, lo + o:hi + o]).sum(-1) / np.sqrt(D)
    e = np.exp(scores - scores.max(-1, keepdims=True))
    return e / e.sum(-1, keepdims=True)

@@ -1,0 +1,222 @@
+import math
+from contextlib import ExitStack
+
+import concourse.mybir as mybir
+from concourse.masks import make_identity
+
+F32 = mybir.dt.float32
+BF16 = mybir.dt.bfloat16
+I32 = mybir.dt.int32
+U32 = mybir.dt.uint32
+U8 = mybir.dt.uint8
+FP8X4 = mybir.dt.float8_e4m3fn_x4
+FP4X4 = mybir.dt.float4_e2m1fn_x4
+ALU = mybir.AluOpType
+ACT = mybir.ActivationFunctionType
+AXIS_X = mybir.AxisListType.X
+
+P = 128
+TOKENS = 32 * 256
+SEQ = 256
+D = 512
+STEPS = TOKENS // P
+PARTS_PER_SEQ = SEQ // STEPS
+HALO = 2
+BAND = 2 * HALO + 1
+CHUNK = 8
+CHUNKS = STEPS // CHUNK
+PAIR = 2
+SCORE_PAD = 8
+GPSIMD_EVERY = 4
+BIAS_GROUP = 4
+INV_SQRT_D = 1.0 / math.sqrt(D)
+MASKED = -1.0e30
+
+FLOPS = 2 * TOKENS * D * D + 2 * TOKENS * BAND * D
+
+
+def tile_crosssliceattention_pa_t_kernel(tc, x, Wq_words, Wq_scales, bq, k_proj, out):
+    nc = tc.nc
+    x_steps = x.flatten_outer_dims().rearrange("(p t) k -> p t k", t=STEPS)
+    k_steps = k_proj.flatten_outer_dims().rearrange("(p t) d -> p t d", t=STEPS)
+    out_rows = out.flatten_outer_dims().rearrange("(p t) j -> p (t j)", t=STEPS)
+
+    with ExitStack() as stack:
+        keep = stack.enter_context(tc.tile_pool(name="keep", bufs=1))
+        x_pool = stack.enter_context(tc.tile_pool(name="x_pool", bufs=4))
+        quant = stack.enter_context(tc.tile_pool(name="quant", bufs=2))
+        work = stack.enter_context(tc.tile_pool(name="work", bufs=2))
+        junk_pool = stack.enter_context(tc.tile_pool(name="junk_pool", bufs=4))
+        psum_t = stack.enter_context(tc.psum_pool(name="psum_t", bufs=2))
+        psum_q = stack.enter_context(tc.psum_pool(name="psum_q", bufs=4))
+
+        w_words = keep.tile([P, 2 * D], U8, align_bytes=64)
+        w_plane = keep.tile([P, D], U8, align_bytes=64)
+        bias_rows = keep.tile([P, D], BF16)
+        ident = keep.tile([P, P], F32)
+        k_ext = keep.tile([P, STEPS + 2 * HALO, D], BF16)
+        raw = keep.tile([P, STEPS, SCORE_PAD], F32)
+        bias_dot = keep.tile([P, STEPS + 2 * HALO], F32)
+
+        nc.vector.memset(w_plane[:].bitcast(I32), 0)
+        nc.vector.memset(k_ext[:, 0:HALO, :], 0.0)
+        nc.vector.memset(k_ext[:, STEPS + HALO :, :], 0.0)
+        make_identity(nc, ident[:])
+
+        warm = keep.tile([P, 1], F32)
+        nc.vector.memset(warm[:], 0.0)
+        nc.scalar.activation(out=warm[:], in_=warm[:], func=ACT.Exp)
+
+        def load_x(c):
+            x_chunk = x_pool.tile([P, CHUNK, D], BF16, name="x_chunk")
+            nc.sync.dma_start(out=x_chunk[:], in_=x_steps[:, c * CHUNK : (c + 1) * CHUNK, :])
+            return x_chunk
+
+        def load_k(c):
+            nc.sync.dma_start(
+                out=k_ext[:, HALO + c * CHUNK : HALO + (c + 1) * CHUNK, :],
+                in_=k_steps[:, c * CHUNK : (c + 1) * CHUNK, :],
+            )
+
+        x_chunks = {0: load_x(0)}
+        nc.sync.dma_start(out=w_words[:].bitcast(I32), in_=Wq_words[0].bitcast(I32))
+        for quadrant in range(4):
+            nc.sync.dma_start(
+                out=w_plane[32 * quadrant : 32 * quadrant + 4, :].bitcast(I32),
+                in_=Wq_scales[0, 4 * quadrant : 4 * quadrant + 4, :].bitcast(I32),
+            )
+        nc.scalar.dma_start(out=k_ext[1:16, 0:HALO, :], in_=k_steps[0:15, STEPS - HALO :, :])
+        nc.scalar.dma_start(out=k_ext[16:P, 0:HALO, :], in_=k_steps[15 : P - 1, STEPS - HALO :, :])
+        load_k(0)
+        nc.scalar.dma_start(out=bias_rows[:], in_=bq.partition_broadcast(P))
+        nc.scalar.dma_start(out=k_ext[0:112, STEPS + HALO :, :], in_=k_steps[1:113, 0:HALO, :])
+        nc.scalar.dma_start(out=k_ext[112 : P - 1, STEPS + HALO :, :], in_=k_steps[113:P, 0:HALO, :])
+
+        neg = keep.tile([P, PARTS_PER_SEQ], F32)
+        nc.vector.tensor_reduce(
+            out=neg[:],
+            in_=ident[:].rearrange("p (b c) -> p c b", c=PARTS_PER_SEQ),
+            axis=AXIS_X,
+            op=ALU.add,
+        )
+        nc.vector.tensor_scalar_mul(out=neg[:], in0=neg[:], scalar1=MASKED)
+
+        def quantise_chunk(x_chunk):
+            x_words = x_chunk[:].rearrange("p t k -> p (t k)").bitcast(F32)
+            x_words = x_words.rearrange("p (t w) -> p t w", t=CHUNK)
+            grouped = quant.tile([P, CHUNK * P * 4], BF16, align_bytes=64, name="grouped")
+            grouped_words = grouped[:].bitcast(F32).rearrange(
+                "q (t p u) -> q t p u", t=CHUNK, u=2
+            )
+            for first in range(0, CHUNK, PAIR):
+                xt = psum_t.tile([P, PAIR, 2, P], F32, name="xt")
+                for i in range(PAIR):
+                    for u in range(2):
+                        nc.tensor.transpose(xt[:, i, u, :], x_words[:, first + i, u : D // 2 : 2], ident[:])
+                nc.scalar.copy(
+                    out=grouped_words[:, first : first + PAIR, :, :],
+                    in_=xt[:].rearrange("q t u p -> q t p u"),
+                )
+            codes = quant.tile([P, CHUNK * P], U32, align_bytes=64, name="codes")
+            scales = quant.tile([P, CHUNK * P], U8, align_bytes=64, name="scales")
+            nc.vector.quantize_mx(out=codes[:].bitcast(FP8X4), scales=scales[:], in_=grouped[:])
+            return codes, scales
+
+        def sum_on_scalar(products, sums):
+            nc.scalar.activation(
+                out=products, in_=products, func=ACT.Copy, scale=INV_SQRT_D, accum_out=sums
+            )
+
+        def scores_of_step(t, codes, scales):
+            cols = slice((t % CHUNK) * P, (t % CHUNK + 1) * P)
+            q_ps = psum_q.tile([P, D], F32, name="q_ps")
+            nc.tensor.matmul_mx(
+                out=q_ps[:],
+                lhsT=codes[:, cols].bitcast(FP8X4),
+                lhsT_scale=scales[:, cols],
+                rhs=w_words[:].bitcast(FP4X4),
+                rhs_scale=w_plane[:],
+                start=True,
+                stop=True,
+            )
+            if t % GPSIMD_EVERY == GPSIMD_EVERY - 1:
+                q_sb = work.tile([P, D], F32, name="q_sb")
+                nc.scalar.copy(out=q_sb[:], in_=q_ps[:])
+                products = work.tile([P, BAND, D], F32, name="products")
+                nc.gpsimd.tensor_tensor(
+                    out=products[:],
+                    in0=q_sb[:].unsqueeze(1).to_broadcast([P, BAND, D]),
+                    in1=k_ext[:, t : t + BAND, :],
+                    op=ALU.mult,
+                )
+                for j in range(BAND):
+                    sum_on_scalar(products[:, j, :], raw[:, t, j : j + 1])
+            else:
+                for j in range(BAND):
+                    junk = junk_pool.tile([P, D], F32, name="junk")
+                    nc.vector.scalar_tensor_tensor(
+                        out=junk[:],
+                        in0=q_ps[:],
+                        scalar=INV_SQRT_D,
+                        in1=k_ext[:, t + j, :],
+                        op0=ALU.mult,
+                        op1=ALU.mult,
+                        accum_out=raw[:, t, j : j + 1],
+                    )
+
+        def bias_dots(first):
+            bias_products = work.tile([P, BIAS_GROUP, D], F32, name="bias_products")
+            nc.gpsimd.tensor_tensor(
+                out=bias_products[:],
+                in0=k_ext[:, first : first + BIAS_GROUP, :],
+                in1=bias_rows[:].unsqueeze(1).to_broadcast([P, BIAS_GROUP, D]),
+                op=ALU.mult,
+            )
+            for i in range(BIAS_GROUP):
+                sum_on_scalar(bias_products[:, i, :], bias_dot[:, first + i : first + i + 1])
+
+        quantised = {0: quantise_chunk(x_chunks[0])}
+        for c in range(CHUNKS):
+            if c + 1 < CHUNKS:
+                x_chunks[c + 1] = load_x(c + 1)
+                load_k(c + 1)
+                quantised[c + 1] = quantise_chunk(x_chunks[c + 1])
+            codes, scales = quantised[c]
+            for t in range(c * CHUNK, (c + 1) * CHUNK):
+                scores_of_step(t, codes, scales)
+            for first in range(c * CHUNK, (c + 1) * CHUNK, BIAS_GROUP):
+                bias_dots(first)
+        bias_dots(STEPS)
+
+        scores = keep.tile([P, STEPS, BAND], F32)
+        for j in range(BAND):
+            nc.vector.tensor_tensor(
+                out=scores[:, :, j], in0=raw[:, :, j], in1=bias_dot[:, j : j + STEPS], op=ALU.add
+            )
+        for i in range(HALO):
+            low = scores[:, i, 0 : HALO - i]
+            nc.vector.tensor_scalar_add(out=low, in0=low, scalar1=neg[:, 0:1])
+            high = scores[:, STEPS - 1 - i, BAND - HALO + i : BAND]
+            nc.vector.tensor_scalar_add(
+                out=high, in0=high, scalar1=neg[:, PARTS_PER_SEQ - 1 : PARTS_PER_SEQ]
+            )
+        top = keep.tile([P, STEPS], F32)
+        nc.vector.tensor_reduce(out=top[:], in_=scores[:], axis=AXIS_X, op=ALU.max)
+        weights = keep.tile([P, STEPS, BAND], F32)
+        nc.vector.tensor_tensor(
+            out=weights[:],
+            in0=scores[:],
+            in1=top[:].unsqueeze(2).to_broadcast([P, STEPS, BAND]),
+            op=ALU.subtract,
+        )
+        nc.scalar.activation(out=weights[:], in_=weights[:], func=ACT.Exp)
+        total = keep.tile([P, STEPS], F32)
+        nc.vector.tensor_reduce(out=total[:], in_=weights[:], axis=AXIS_X, op=ALU.add)
+        nc.vector.reciprocal(out=total[:], in_=total[:])
+        nc.vector.tensor_tensor(
+            out=weights[:],
+            in0=weights[:],
+            in1=total[:].unsqueeze(2).to_broadcast([P, STEPS, BAND]),
+            op=ALU.mult,
+        )
+        nc.sync.dma_start(out=out_rows, in_=weights[:].rearrange("p t j -> p (t j)"))

@@ -19,16 +19,17 @@ P = 128
 TOKENS = 32 * 256
 SEQ = 256
 D = 512
+D_BLOCKS = D // P
 STEPS = TOKENS // P
 PARTS_PER_SEQ = SEQ // STEPS
 HALO = 2
 BAND = 2 * HALO + 1
-CHUNK = 8
-CHUNKS = STEPS // CHUNK
+ROWS = STEPS + 2 * HALO
+GROUP = 4
+GROUPS = STEPS // GROUP
 PAIR = 2
 SCORE_PAD = 8
-GPSIMD_EVERY = 4
-BIAS_GROUP = 4
+GPSIMD_EVERY = 3
 INV_SQRT_D = 1.0 / math.sqrt(D)
 MASKED = -1.0e30
 
@@ -42,56 +43,35 @@ def tile_crosssliceattention_pa_t_kernel(tc, x, Wq_words, Wq_scales, bq, k_proj,
     out_rows = out.flatten_outer_dims().rearrange("(p t) j -> p (t j)", t=STEPS)
 
     with ExitStack() as stack:
+        stack.enter_context(tc.manual_schedule())
         keep = stack.enter_context(tc.tile_pool(name="keep", bufs=1))
-        x_pool = stack.enter_context(tc.tile_pool(name="x_pool", bufs=4))
-        quant = stack.enter_context(tc.tile_pool(name="quant", bufs=2))
+        quant = stack.enter_context(tc.tile_pool(name="quant", bufs=3))
         work = stack.enter_context(tc.tile_pool(name="work", bufs=2))
         junk_pool = stack.enter_context(tc.tile_pool(name="junk_pool", bufs=4))
-        psum_t = stack.enter_context(tc.psum_pool(name="psum_t", bufs=2))
-        psum_q = stack.enter_context(tc.psum_pool(name="psum_q", bufs=4))
+        psum_x = stack.enter_context(tc.psum_pool(name="psum_x", bufs=2))
+        psum_k = stack.enter_context(tc.psum_pool(name="psum_k", bufs=2))
+        psum_q = stack.enter_context(tc.psum_pool(name="psum_q", bufs=3))
+        psum_b = stack.enter_context(tc.psum_pool(name="psum_b", bufs=1))
 
         w_words = keep.tile([P, 2 * D], U8, align_bytes=64)
         w_plane = keep.tile([P, D], U8, align_bytes=64)
-        bias_rows = keep.tile([P, D], BF16)
         ident = keep.tile([P, P], F32)
-        k_ext = keep.tile([P, STEPS + 2 * HALO, D], BF16)
+        ident_bf = keep.tile([P, P], BF16)
+        bias_rows = keep.tile([P, P], BF16)
+        bias_cols = keep.tile([P, D_BLOCKS], BF16)
+        x_all = keep.tile([P, STEPS, D], BF16)
+        k_ext = keep.tile([P, ROWS, D], BF16)
         raw = keep.tile([P, STEPS, SCORE_PAD], F32)
-        bias_dot = keep.tile([P, STEPS + 2 * HALO], F32)
+        bias_dot = psum_b.tile([P, ROWS], F32)
 
         nc.vector.memset(w_plane[:].bitcast(I32), 0)
         nc.vector.memset(k_ext[:, 0:HALO, :], 0.0)
         nc.vector.memset(k_ext[:, STEPS + HALO :, :], 0.0)
-        make_identity(nc, ident[:])
-
+        nc.vector.memset(bias_rows[:], 0.0)
         warm = keep.tile([P, 1], F32)
         nc.vector.memset(warm[:], 0.0)
-        nc.scalar.activation(out=warm[:], in_=warm[:], func=ACT.Exp)
-
-        def load_x(c):
-            x_chunk = x_pool.tile([P, CHUNK, D], BF16, name="x_chunk")
-            nc.sync.dma_start(out=x_chunk[:], in_=x_steps[:, c * CHUNK : (c + 1) * CHUNK, :])
-            return x_chunk
-
-        def load_k(c):
-            nc.sync.dma_start(
-                out=k_ext[:, HALO + c * CHUNK : HALO + (c + 1) * CHUNK, :],
-                in_=k_steps[:, c * CHUNK : (c + 1) * CHUNK, :],
-            )
-
-        x_chunks = {0: load_x(0)}
-        nc.sync.dma_start(out=w_words[:].bitcast(I32), in_=Wq_words[0].bitcast(I32))
-        for quadrant in range(4):
-            nc.sync.dma_start(
-                out=w_plane[32 * quadrant : 32 * quadrant + 4, :].bitcast(I32),
-                in_=Wq_scales[0, 4 * quadrant : 4 * quadrant + 4, :].bitcast(I32),
-            )
-        nc.scalar.dma_start(out=k_ext[1:16, 0:HALO, :], in_=k_steps[0:15, STEPS - HALO :, :])
-        nc.scalar.dma_start(out=k_ext[16:P, 0:HALO, :], in_=k_steps[15 : P - 1, STEPS - HALO :, :])
-        load_k(0)
-        nc.scalar.dma_start(out=bias_rows[:], in_=bq.partition_broadcast(P))
-        nc.scalar.dma_start(out=k_ext[0:112, STEPS + HALO :, :], in_=k_steps[1:113, 0:HALO, :])
-        nc.scalar.dma_start(out=k_ext[112 : P - 1, STEPS + HALO :, :], in_=k_steps[113:P, 0:HALO, :])
-
+        make_identity(nc, ident[:])
+        nc.vector.tensor_copy(out=ident_bf[:], in_=ident[:])
         neg = keep.tile([P, PARTS_PER_SEQ], F32)
         nc.vector.tensor_reduce(
             out=neg[:],
@@ -100,35 +80,71 @@ def tile_crosssliceattention_pa_t_kernel(tc, x, Wq_words, Wq_scales, bq, k_proj,
             op=ALU.add,
         )
         nc.vector.tensor_scalar_mul(out=neg[:], in0=neg[:], scalar1=MASKED)
+        nc.scalar.activation(out=warm[:], in_=warm[:], func=ACT.Exp)
 
-        def quantise_chunk(x_chunk):
-            x_words = x_chunk[:].rearrange("p t k -> p (t k)").bitcast(F32)
-            x_words = x_words.rearrange("p (t w) -> p t w", t=CHUNK)
-            grouped = quant.tile([P, CHUNK * P * 4], BF16, align_bytes=64, name="grouped")
-            grouped_words = grouped[:].bitcast(F32).rearrange(
-                "q (t p u) -> q t p u", t=CHUNK, u=2
-            )
-            for first in range(0, CHUNK, PAIR):
-                xt = psum_t.tile([P, PAIR, 2, P], F32, name="xt")
-                for i in range(PAIR):
-                    for u in range(2):
-                        nc.tensor.transpose(xt[:, i, u, :], x_words[:, first + i, u : D // 2 : 2], ident[:])
-                nc.scalar.copy(
-                    out=grouped_words[:, first : first + PAIR, :, :],
-                    in_=xt[:].rearrange("q t u p -> q t p u"),
-                )
-            codes = quant.tile([P, CHUNK * P], U32, align_bytes=64, name="codes")
-            scales = quant.tile([P, CHUNK * P], U8, align_bytes=64, name="scales")
-            nc.vector.quantize_mx(out=codes[:].bitcast(FP8X4), scales=scales[:], in_=grouped[:])
-            return codes, scales
+        def load_x(m):
+            steps = slice(m * GROUP, (m + 1) * GROUP)
+            nc.sync.dma_start(out=x_all[:, steps, :], in_=x_steps[:, steps, :])
 
-        def sum_on_scalar(products, sums):
-            nc.scalar.activation(
-                out=products, in_=products, func=ACT.Copy, scale=INV_SQRT_D, accum_out=sums
+        def load_k(m):
+            nc.sync.dma_start(
+                out=k_ext[:, HALO + m * GROUP : HALO + (m + 1) * GROUP, :],
+                in_=k_steps[:, m * GROUP : (m + 1) * GROUP, :],
             )
 
-        def scores_of_step(t, codes, scales):
-            cols = slice((t % CHUNK) * P, (t % CHUNK + 1) * P)
+        load_x(0)
+        nc.sync.dma_start(out=w_words[:].bitcast(I32), in_=Wq_words[0].bitcast(I32))
+        for quadrant in range(4):
+            nc.sync.dma_start(
+                out=w_plane[32 * quadrant : 32 * quadrant + 4, :].bitcast(I32),
+                in_=Wq_scales[0, 4 * quadrant : 4 * quadrant + 4, :].bitcast(I32),
+            )
+        nc.scalar.dma_start(out=k_ext[1:16, 0:HALO, :], in_=k_steps[0:15, STEPS - HALO :, :])
+        nc.scalar.dma_start(out=k_ext[16:P, 0:HALO, :], in_=k_steps[15 : P - 1, STEPS - HALO :, :])
+        nc.scalar.dma_start(
+            out=bias_rows[0:D_BLOCKS, :], in_=bq.rearrange("(c d) -> c d", c=D_BLOCKS)
+        )
+        nc.scalar.dma_start(out=k_ext[0:112, STEPS + HALO :, :], in_=k_steps[1:113, 0:HALO, :])
+        nc.scalar.dma_start(out=k_ext[112 : P - 1, STEPS + HALO :, :], in_=k_steps[113:P, 0:HALO, :])
+        load_x(1)
+        load_k(0)
+        load_k(1)
+        for m in range(2, GROUPS):
+            load_x(m)
+            load_k(m)
+
+        x_words = x_all[:].rearrange("p t k -> p (t k)").bitcast(F32)
+        x_words = x_words.rearrange("p (t w) -> p t w", t=STEPS)
+        grouped_of = {}
+        quantised_of = {}
+
+        def transpose_x_pair(first):
+            m = first // GROUP
+            if first % GROUP == 0:
+                grouped_of[m] = quant.tile([P, GROUP * P * 4], BF16, align_bytes=64, name="grouped")
+            grouped_words = grouped_of[m][:].bitcast(F32).rearrange(
+                "q (t p u) -> q t p u", t=GROUP, u=2
+            )
+            xt = psum_x.tile([P, PAIR, 2, P], F32, name="xt")
+            for i in range(PAIR):
+                for u in range(2):
+                    nc.tensor.transpose(xt[:, i, u, :], x_words[:, first + i, u : D // 2 : 2], ident[:])
+            nc.scalar.copy(
+                out=grouped_words[:, first % GROUP : first % GROUP + PAIR, :, :],
+                in_=xt[:].rearrange("q t u p -> q t p u"),
+            )
+
+        def quantise_group(m):
+            codes = quant.tile([P, GROUP * P], U32, align_bytes=64, name="codes")
+            scales = quant.tile([P, GROUP * P], U8, align_bytes=64, name="scales")
+            nc.vector.quantize_mx(
+                out=codes[:].bitcast(FP8X4), scales=scales[:], in_=grouped_of[m][:]
+            )
+            quantised_of[m] = (codes, scales)
+
+        def project(t):
+            codes, scales = quantised_of[t // GROUP]
+            cols = slice((t % GROUP) * P, (t % GROUP + 1) * P)
             q_ps = psum_q.tile([P, D], F32, name="q_ps")
             nc.tensor.matmul_mx(
                 out=q_ps[:],
@@ -139,59 +155,108 @@ def tile_crosssliceattention_pa_t_kernel(tc, x, Wq_words, Wq_scales, bq, k_proj,
                 start=True,
                 stop=True,
             )
-            if t % GPSIMD_EVERY == GPSIMD_EVERY - 1:
-                q_sb = work.tile([P, D], F32, name="q_sb")
-                nc.scalar.copy(out=q_sb[:], in_=q_ps[:])
-                products = work.tile([P, BAND, D], F32, name="products")
-                nc.gpsimd.tensor_tensor(
-                    out=products[:],
-                    in0=q_sb[:].unsqueeze(1).to_broadcast([P, BAND, D]),
-                    in1=k_ext[:, t : t + BAND, :],
-                    op=ALU.mult,
-                )
-                for j in range(BAND):
-                    sum_on_scalar(products[:, j, :], raw[:, t, j : j + 1])
-            else:
-                for j in range(BAND):
-                    junk = junk_pool.tile([P, D], F32, name="junk")
-                    nc.vector.scalar_tensor_tensor(
-                        out=junk[:],
-                        in0=q_ps[:],
-                        scalar=INV_SQRT_D,
-                        in1=k_ext[:, t + j, :],
-                        op0=ALU.mult,
-                        op1=ALU.mult,
-                        accum_out=raw[:, t, j : j + 1],
-                    )
+            return q_ps
 
-        def bias_dots(first):
-            bias_products = work.tile([P, BIAS_GROUP, D], F32, name="bias_products")
+        def scores_on_vector(t, q_ps):
+            for j in range(BAND):
+                junk = junk_pool.tile([P, D], F32, name="junk")
+                nc.vector.scalar_tensor_tensor(
+                    out=junk[:],
+                    in0=q_ps[:],
+                    scalar=INV_SQRT_D,
+                    in1=k_ext[:, t + j, :],
+                    op0=ALU.mult,
+                    op1=ALU.mult,
+                    accum_out=raw[:, t, j : j + 1],
+                )
+
+        def multiply_on_gpsimd(t, q_ps):
+            q_sb = work.tile([P, D], F32, name="q_sb")
+            nc.scalar.copy(out=q_sb[:], in_=q_ps[:])
+            products = work.tile([P, BAND, D], F32, name="products")
             nc.gpsimd.tensor_tensor(
-                out=bias_products[:],
-                in0=k_ext[:, first : first + BIAS_GROUP, :],
-                in1=bias_rows[:].unsqueeze(1).to_broadcast([P, BIAS_GROUP, D]),
+                out=products[:],
+                in0=q_sb[:].unsqueeze(1).to_broadcast([P, BAND, D]),
+                in1=k_ext[:, t : t + BAND, :],
                 op=ALU.mult,
             )
-            for i in range(BIAS_GROUP):
-                sum_on_scalar(bias_products[:, i, :], bias_dot[:, first + i : first + i + 1])
+            return products
 
-        quantised = {0: quantise_chunk(x_chunks[0])}
-        for c in range(CHUNKS):
-            if c + 1 < CHUNKS:
-                x_chunks[c + 1] = load_x(c + 1)
-                load_k(c + 1)
-                quantised[c + 1] = quantise_chunk(x_chunks[c + 1])
-            codes, scales = quantised[c]
-            for t in range(c * CHUNK, (c + 1) * CHUNK):
-                scores_of_step(t, codes, scales)
-            for first in range(c * CHUNK, (c + 1) * CHUNK, BIAS_GROUP):
-                bias_dots(first)
-        bias_dots(STEPS)
+        def sum_on_scalar(t, products):
+            for j in range(BAND):
+                nc.scalar.activation(
+                    out=products[:, j, :],
+                    in_=products[:, j, :],
+                    func=ACT.Copy,
+                    scale=INV_SQRT_D,
+                    accum_out=raw[:, t, j : j + 1],
+                )
+
+        def transpose_k_pair(first):
+            kt = psum_k.tile([P, PAIR, D_BLOCKS, P], BF16, name="kt")
+            for i in range(PAIR):
+                for c in range(D_BLOCKS):
+                    nc.tensor.transpose(kt[:, i, c, :], k_ext[:, first + i, c * P : (c + 1) * P], ident_bf[:])
+            kt_sb = work.tile([P, PAIR, D_BLOCKS, P], BF16, name="kt_sb")
+            nc.scalar.copy(out=kt_sb[:], in_=kt[:])
+            return kt_sb
+
+        def bias_dot_pair(first, kt_sb):
+            for i in range(PAIR):
+                for c in range(D_BLOCKS):
+                    nc.tensor.matmul(
+                        out=bias_dot[:, first + i : first + i + 1],
+                        lhsT=kt_sb[:, i, c, :],
+                        rhs=bias_cols[:, c : c + 1],
+                        start=(c == 0),
+                        stop=(c == D_BLOCKS - 1),
+                    )
+
+        for first in range(0, 2 * GROUP, PAIR):
+            transpose_x_pair(first)
+        quantise_group(0)
+        bias_t = psum_k.tile([P, PAIR, D_BLOCKS, P], BF16, name="kt")
+        nc.tensor.transpose(bias_t[:, 0, 0, :], bias_rows[:], ident_bf[:])
+        nc.scalar.copy(out=bias_cols[:], in_=bias_t[:, 0, 0, 0:D_BLOCKS])
+
+        waiting_rows = []
+        waiting_products = []
+
+        def bias_term_of_rows(first):
+            waiting_rows.append((first, transpose_k_pair(first)))
+            if len(waiting_rows) > 1:
+                bias_dot_pair(*waiting_rows.pop(0))
+
+        for m in range(GROUPS):
+            if m + 1 < GROUPS:
+                quantise_group(m + 1)
+            for t in range(m * GROUP, (m + 1) * GROUP):
+                q_ps = project(t)
+                on_gpsimd = t % GPSIMD_EVERY == 1
+                if on_gpsimd:
+                    waiting_products.append((t, multiply_on_gpsimd(t, q_ps)))
+                    if len(waiting_products) > 1:
+                        sum_on_scalar(*waiting_products.pop(0))
+                if t % PAIR == 1:
+                    bias_term_of_rows(t - 1)
+                elif t + 2 * GROUP < STEPS:
+                    transpose_x_pair(t + 2 * GROUP)
+                elif t + 2 * GROUP < ROWS:
+                    bias_term_of_rows(t + 2 * GROUP)
+                if not on_gpsimd:
+                    scores_on_vector(t, q_ps)
+        bias_dot_pair(*waiting_rows.pop(0))
+        sum_on_scalar(*waiting_products.pop(0))
 
         scores = keep.tile([P, STEPS, BAND], F32)
         for j in range(BAND):
-            nc.vector.tensor_tensor(
-                out=scores[:, :, j], in0=raw[:, :, j], in1=bias_dot[:, j : j + STEPS], op=ALU.add
+            nc.vector.scalar_tensor_tensor(
+                out=scores[:, :, j],
+                in0=bias_dot[:, j : j + STEPS],
+                scalar=INV_SQRT_D,
+                in1=raw[:, :, j],
+                op0=ALU.mult,
+                op1=ALU.add,
             )
         for i in range(HALO):
             low = scores[:, i, 0 : HALO - i]

@@ -48,9 +48,8 @@ def tile_crosssliceattention_pa_t_kernel(tc, x, Wq_words, Wq_scales, bq, k_proj,
         quant = stack.enter_context(tc.tile_pool(name="quant", bufs=3))
         work = stack.enter_context(tc.tile_pool(name="work", bufs=2))
         junk_pool = stack.enter_context(tc.tile_pool(name="junk_pool", bufs=4))
-        psum_x = stack.enter_context(tc.psum_pool(name="psum_x", bufs=2))
-        psum_k = stack.enter_context(tc.psum_pool(name="psum_k", bufs=2))
-        psum_q = stack.enter_context(tc.psum_pool(name="psum_q", bufs=3))
+        psum_t = stack.enter_context(tc.psum_pool(name="psum_t", bufs=3))
+        psum_q = stack.enter_context(tc.psum_pool(name="psum_q", bufs=4))
         psum_b = stack.enter_context(tc.psum_pool(name="psum_b", bufs=1))
 
         w_words = keep.tile([P, 2 * D], U8, align_bytes=64)
@@ -125,7 +124,7 @@ def tile_crosssliceattention_pa_t_kernel(tc, x, Wq_words, Wq_scales, bq, k_proj,
             grouped_words = grouped_of[m][:].bitcast(F32).rearrange(
                 "q (t p u) -> q t p u", t=GROUP, u=2
             )
-            xt = psum_x.tile([P, PAIR, 2, P], F32, name="xt")
+            xt = psum_t.tile([P, PAIR, 2, P], F32, name="xt", tag="transposed")
             for i in range(PAIR):
                 for u in range(2):
                     nc.tensor.transpose(xt[:, i, u, :], x_words[:, first + i, u : D // 2 : 2], ident[:])
@@ -193,7 +192,7 @@ def tile_crosssliceattention_pa_t_kernel(tc, x, Wq_words, Wq_scales, bq, k_proj,
                 )
 
         def transpose_k_pair(first):
-            kt = psum_k.tile([P, PAIR, D_BLOCKS, P], BF16, name="kt")
+            kt = psum_t.tile([P, PAIR, D_BLOCKS, P], BF16, name="kt", tag="transposed")
             for i in range(PAIR):
                 for c in range(D_BLOCKS):
                     nc.tensor.transpose(kt[:, i, c, :], k_ext[:, first + i, c * P : (c + 1) * P], ident_bf[:])
@@ -215,7 +214,7 @@ def tile_crosssliceattention_pa_t_kernel(tc, x, Wq_words, Wq_scales, bq, k_proj,
         for first in range(0, 2 * GROUP, PAIR):
             transpose_x_pair(first)
         quantise_group(0)
-        bias_t = psum_k.tile([P, PAIR, D_BLOCKS, P], BF16, name="kt")
+        bias_t = psum_t.tile([P, PAIR, D_BLOCKS, P], BF16, name="bias_t", tag="transposed")
         nc.tensor.transpose(bias_t[:, 0, 0, :], bias_rows[:], ident_bf[:])
         nc.scalar.copy(out=bias_cols[:], in_=bias_t[:, 0, 0, 0:D_BLOCKS])
 
@@ -230,21 +229,22 @@ def tile_crosssliceattention_pa_t_kernel(tc, x, Wq_words, Wq_scales, bq, k_proj,
         for m in range(GROUPS):
             if m + 1 < GROUPS:
                 quantise_group(m + 1)
-            for t in range(m * GROUP, (m + 1) * GROUP):
-                q_ps = project(t)
-                on_gpsimd = t % GPSIMD_EVERY == 1
-                if on_gpsimd:
-                    waiting_products.append((t, multiply_on_gpsimd(t, q_ps)))
-                    if len(waiting_products) > 1:
-                        sum_on_scalar(*waiting_products.pop(0))
-                if t % PAIR == 1:
-                    bias_term_of_rows(t - 1)
-                elif t + 2 * GROUP < STEPS:
-                    transpose_x_pair(t + 2 * GROUP)
-                elif t + 2 * GROUP < ROWS:
-                    bias_term_of_rows(t + 2 * GROUP)
-                if not on_gpsimd:
-                    scores_on_vector(t, q_ps)
+            for first in range(m * GROUP, (m + 1) * GROUP, PAIR):
+                pair = range(first, first + PAIR)
+                q_of = {t: project(t) for t in pair}
+                for t in pair:
+                    if t % GPSIMD_EVERY == 1:
+                        waiting_products.append((t, multiply_on_gpsimd(t, q_of[t])))
+                        if len(waiting_products) > 1:
+                            sum_on_scalar(*waiting_products.pop(0))
+                if first + 2 * GROUP < STEPS:
+                    transpose_x_pair(first + 2 * GROUP)
+                elif first + 2 * GROUP < ROWS:
+                    bias_term_of_rows(first + 2 * GROUP)
+                bias_term_of_rows(first)
+                for t in pair:
+                    if t % GPSIMD_EVERY != 1:
+                        scores_on_vector(t, q_of[t])
         bias_dot_pair(*waiting_rows.pop(0))
         sum_on_scalar(*waiting_products.pop(0))
 

@@ -29,7 +29,7 @@ GROUP = 4
 GROUPS = STEPS // GROUP
 PAIR = 2
 SCORE_PAD = 8
-GPSIMD_EVERY = 3
+GPSIMD_EVERY = 4
 INV_SQRT_D = 1.0 / math.sqrt(D)
 MASKED = -1.0e30
 
@@ -48,8 +48,9 @@ def tile_crosssliceattention_pa_t_kernel(tc, x, Wq_words, Wq_scales, bq, k_proj,
         quant = stack.enter_context(tc.tile_pool(name="quant", bufs=3))
         work = stack.enter_context(tc.tile_pool(name="work", bufs=2))
         junk_pool = stack.enter_context(tc.tile_pool(name="junk_pool", bufs=4))
-        psum_t = stack.enter_context(tc.psum_pool(name="psum_t", bufs=3))
-        psum_q = stack.enter_context(tc.psum_pool(name="psum_q", bufs=4))
+        psum_x = stack.enter_context(tc.psum_pool(name="psum_x", bufs=2))
+        psum_k = stack.enter_context(tc.psum_pool(name="psum_k", bufs=2))
+        psum_q = stack.enter_context(tc.psum_pool(name="psum_q", bufs=3))
         psum_b = stack.enter_context(tc.psum_pool(name="psum_b", bufs=1))
 
         w_words = keep.tile([P, 2 * D], U8, align_bytes=64)
@@ -124,7 +125,7 @@ def tile_crosssliceattention_pa_t_kernel(tc, x, Wq_words, Wq_scales, bq, k_proj,
             grouped_words = grouped_of[m][:].bitcast(F32).rearrange(
                 "q (t p u) -> q t p u", t=GROUP, u=2
             )
-            xt = psum_t.tile([P, PAIR, 2, P], F32, name="xt", tag="transposed")
+            xt = psum_x.tile([P, PAIR, 2, P], F32, name="xt")
             for i in range(PAIR):
                 for u in range(2):
                     nc.tensor.transpose(xt[:, i, u, :], x_words[:, first + i, u : D // 2 : 2], ident[:])
@@ -192,7 +193,7 @@ def tile_crosssliceattention_pa_t_kernel(tc, x, Wq_words, Wq_scales, bq, k_proj,
                 )
 
         def transpose_k_pair(first):
-            kt = psum_t.tile([P, PAIR, D_BLOCKS, P], BF16, name="kt", tag="transposed")
+            kt = psum_k.tile([P, PAIR, D_BLOCKS, P], BF16, name="kt")
             for i in range(PAIR):
                 for c in range(D_BLOCKS):
                     nc.tensor.transpose(kt[:, i, c, :], k_ext[:, first + i, c * P : (c + 1) * P], ident_bf[:])
@@ -214,7 +215,7 @@ def tile_crosssliceattention_pa_t_kernel(tc, x, Wq_words, Wq_scales, bq, k_proj,
         for first in range(0, 2 * GROUP, PAIR):
             transpose_x_pair(first)
         quantise_group(0)
-        bias_t = psum_t.tile([P, PAIR, D_BLOCKS, P], BF16, name="bias_t", tag="transposed")
+        bias_t = psum_k.tile([P, PAIR, D_BLOCKS, P], BF16, name="kt")
         nc.tensor.transpose(bias_t[:, 0, 0, :], bias_rows[:], ident_bf[:])
         nc.scalar.copy(out=bias_cols[:], in_=bias_t[:, 0, 0, 0:D_BLOCKS])
 
@@ -229,22 +230,21 @@ def tile_crosssliceattention_pa_t_kernel(tc, x, Wq_words, Wq_scales, bq, k_proj,
         for m in range(GROUPS):
             if m + 1 < GROUPS:
                 quantise_group(m + 1)
-            for first in range(m * GROUP, (m + 1) * GROUP, PAIR):
-                pair = range(first, first + PAIR)
-                q_of = {t: project(t) for t in pair}
-                for t in pair:
-                    if t % GPSIMD_EVERY == 1:
-                        waiting_products.append((t, multiply_on_gpsimd(t, q_of[t])))
-                        if len(waiting_products) > 1:
-                            sum_on_scalar(*waiting_products.pop(0))
-                if first + 2 * GROUP < STEPS:
-                    transpose_x_pair(first + 2 * GROUP)
-                elif first + 2 * GROUP < ROWS:
-                    bias_term_of_rows(first + 2 * GROUP)
-                bias_term_of_rows(first)
-                for t in pair:
-                    if t % GPSIMD_EVERY != 1:
-                        scores_on_vector(t, q_of[t])
+            for t in range(m * GROUP, (m + 1) * GROUP):
+                q_ps = project(t)
+                on_gpsimd = t % GPSIMD_EVERY == 1
+                if on_gpsimd:
+                    waiting_products.append((t, multiply_on_gpsimd(t, q_ps)))
+                    if len(waiting_products) > 1:
+                        sum_on_scalar(*waiting_products.pop(0))
+                if t % PAIR == 1:
+                    bias_term_of_rows(t - 1)
+                elif t + 2 * GROUP < STEPS:
+                    transpose_x_pair(t + 2 * GROUP)
+                elif t + 2 * GROUP < ROWS:
+                    bias_term_of_rows(t + 2 * GROUP)
+                if not on_gpsimd:
+                    scores_on_vector(t, q_ps)
         bias_dot_pair(*waiting_rows.pop(0))
         sum_on_scalar(*waiting_products.pop(0))
 

@@ -29,7 +29,7 @@ GROUP = 4
 GROUPS = STEPS // GROUP
 PAIR = 2
 SCORE_PAD = 8
-GPSIMD_EVERY = 4
+GPSIMD_EVERY = 3
 INV_SQRT_D = 1.0 / math.sqrt(D)
 MASKED = -1.0e30
 
@@ -174,12 +174,10 @@ def tile_crosssliceattention_pa_t_kernel(tc, x, Wq_words, Wq_scales, bq, k_proj,
             q_sb = work.tile([P, D], F32, name="q_sb")
             nc.scalar.copy(out=q_sb[:], in_=q_ps[:])
             products = work.tile([P, BAND, D], F32, name="products")
-            nc.gpsimd.tensor_tensor(
-                out=products[:],
-                in0=q_sb[:].unsqueeze(1).to_broadcast([P, BAND, D]),
-                in1=k_ext[:, t : t + BAND, :],
-                op=ALU.mult,
-            )
+            for j in range(BAND):
+                nc.gpsimd.tensor_tensor(
+                    out=products[:, j, :], in0=q_sb[:], in1=k_ext[:, t + j, :], op=ALU.mult
+                )
             return products
 
         def sum_on_scalar(t, products):

@@ -20,37 +20,61 @@ TOKENS = 32 * 256
 SEQ = 256
 D = 512
 D_BLOCKS = D // P
-STEPS = TOKENS // P
-PARTS_PER_SEQ = SEQ // STEPS
 HALO = 2
 BAND = 2 * HALO + 1
-ROWS = STEPS + 2 * HALO
-GROUP = 4
-GROUPS = STEPS // GROUP
-PAIR = 2
-SCORE_PAD = 8
-GPSIMD_EVERY = 3
 INV_SQRT_D = 1.0 / math.sqrt(D)
 MASKED = -1.0e30
+
+BAND_SEQS = 12
+SEQ_TILES = SEQ // P
+BAND_TILES = BAND_SEQS * SEQ_TILES
+BAND_TOKENS = BAND_SEQS * SEQ
+WINDOW = P + 2 * HALO
+SLOTS = BAND + 1
+HALF_TILES = BAND_TILES // 2
+HALF_COLS = P // 2
+BAND_PERIOD = 3
+BAND_START = -4
+
+RUN = (TOKENS - BAND_TOKENS) // P
+ROWS = RUN + 2 * HALO
+GROUP = 4
+GROUPS = RUN // GROUP
+PAIR = 2
+SCORE_PAD = 8
+X_LEAD = 2 * GROUP
+ROWS_LEAD = 3
+GPSIMD_EVERY = 3
+SUM_PLAN = ((2, (0, 1)), (3, (2, 3)), (4, (4,)))
+FIRST_TICK = -X_LEAD
+LAST_TICK = RUN + 2
 
 FLOPS = 2 * TOKENS * D * D + 2 * TOKENS * BAND * D
 
 
 def tile_crosssliceattention_pa_t_kernel(tc, x, Wq_words, Wq_scales, bq, k_proj, out):
     nc = tc.nc
-    x_steps = x.flatten_outer_dims().rearrange("(p t) k -> p t k", t=STEPS)
-    k_steps = k_proj.flatten_outer_dims().rearrange("(p t) d -> p t d", t=STEPS)
-    out_rows = out.flatten_outer_dims().rearrange("(p t) j -> p (t j)", t=STEPS)
+    x_flat = x.flatten_outer_dims()
+    k_flat = k_proj.flatten_outer_dims()
+    out_flat = out.flatten_outer_dims()
+    x_tiles = x_flat[0:BAND_TOKENS, :].rearrange("(i p) k -> p i k", p=P)
+    k_tiles = k_flat[0:BAND_TOKENS, :].rearrange("(i p) d -> p i d", p=P)
+    x_steps = x_flat[BAND_TOKENS:TOKENS, :].rearrange("(p t) k -> p t k", t=RUN)
+    k_steps = k_flat[BAND_TOKENS:TOKENS, :].rearrange("(p t) d -> p t d", t=RUN)
+    k_before = k_flat[BAND_TOKENS - HALO : TOKENS - HALO, :].rearrange("(p t) d -> p t d", t=RUN)
+    k_after = k_flat[BAND_TOKENS + RUN : TOKENS, :].rearrange("(p t) d -> p t d", t=RUN)
+    out_run = out_flat[BAND_TOKENS:TOKENS, :].rearrange("(p t) j -> p (t j)", t=RUN)
 
     with ExitStack() as stack:
         stack.enter_context(tc.manual_schedule())
         keep = stack.enter_context(tc.tile_pool(name="keep", bufs=1))
         quant = stack.enter_context(tc.tile_pool(name="quant", bufs=3))
+        rows_pool = stack.enter_context(tc.tile_pool(name="rows_pool", bufs=3))
         work = stack.enter_context(tc.tile_pool(name="work", bufs=2))
-        junk_pool = stack.enter_context(tc.tile_pool(name="junk_pool", bufs=4))
-        psum_x = stack.enter_context(tc.psum_pool(name="psum_x", bufs=2))
-        psum_k = stack.enter_context(tc.psum_pool(name="psum_k", bufs=2))
+        psum_t = stack.enter_context(tc.psum_pool(name="psum_t", bufs=2))
         psum_q = stack.enter_context(tc.psum_pool(name="psum_q", bufs=3))
+        psum_c = stack.enter_context(tc.psum_pool(name="psum_c", bufs=1))
+        psum_s = stack.enter_context(tc.psum_pool(name="psum_s", bufs=1))
         psum_b = stack.enter_context(tc.psum_pool(name="psum_b", bufs=1))
 
         w_words = keep.tile([P, 2 * D], U8, align_bytes=64)
@@ -58,89 +82,155 @@ def tile_crosssliceattention_pa_t_kernel(tc, x, Wq_words, Wq_scales, bq, k_proj,
         ident = keep.tile([P, P], F32)
         ident_bf = keep.tile([P, P], BF16)
         bias_rows = keep.tile([P, P], BF16)
-        bias_cols = keep.tile([P, D_BLOCKS], BF16)
-        x_all = keep.tile([P, STEPS, D], BF16)
+        bias_pairs = keep.tile([P, 2 * P], BF16)
+        x_run = keep.tile([P, RUN, D], BF16)
         k_ext = keep.tile([P, ROWS, D], BF16)
-        raw = keep.tile([P, STEPS, SCORE_PAD], F32)
+        x_band = keep.tile([P, BAND_TILES, D], BF16)
+        k_band = keep.tile([P, BAND_TILES, D], BF16)
+        raw = keep.tile([P, RUN, SCORE_PAD], F32)
+        slots = keep.tile([P, BAND_TILES, SLOTS], F32)
         bias_dot = psum_b.tile([P, ROWS], F32)
+        key_cols_0 = keep.tile([P, D_BLOCKS, SEQ + 2 * HALO], F32)
+        key_cols_1 = keep.tile([P, D_BLOCKS, SEQ + 2 * HALO], F32)
+        key_cols = [key_cols_0, key_cols_1]
 
         nc.vector.memset(w_plane[:].bitcast(I32), 0)
-        nc.vector.memset(k_ext[:, 0:HALO, :], 0.0)
-        nc.vector.memset(k_ext[:, STEPS + HALO :, :], 0.0)
+        nc.vector.memset(k_ext[:, RUN + HALO :, :], 0.0)
         nc.vector.memset(bias_rows[:], 0.0)
+        nc.vector.memset(bias_pairs[:], 0.0)
         warm = keep.tile([P, 1], F32)
         nc.vector.memset(warm[:], 0.0)
         make_identity(nc, ident[:])
         nc.vector.tensor_copy(out=ident_bf[:], in_=ident[:])
-        neg = keep.tile([P, PARTS_PER_SEQ], F32)
-        nc.vector.tensor_reduce(
-            out=neg[:],
-            in_=ident[:].rearrange("p (b c) -> p c b", c=PARTS_PER_SEQ),
-            axis=AXIS_X,
-            op=ALU.add,
-        )
-        nc.vector.tensor_scalar_mul(out=neg[:], in0=neg[:], scalar1=MASKED)
         nc.scalar.activation(out=warm[:], in_=warm[:], func=ACT.Exp)
+        for cols in key_cols:
+            nc.vector.memset(cols[:, :, 0:HALO], 0.0)
+            nc.vector.memset(cols[:, :, HALO + SEQ :], 0.0)
 
-        def load_x(m):
-            steps = slice(m * GROUP, (m + 1) * GROUP)
-            nc.sync.dma_start(out=x_all[:, steps, :], in_=x_steps[:, steps, :])
-
-        def load_k(m):
-            nc.sync.dma_start(
-                out=k_ext[:, HALO + m * GROUP : HALO + (m + 1) * GROUP, :],
-                in_=k_steps[:, m * GROUP : (m + 1) * GROUP, :],
+        diff_i = keep.tile([P, WINDOW], I32)
+        nc.gpsimd.iota(diff_i[:], pattern=[[1, WINDOW]], base=0, channel_multiplier=-1)
+        diff = keep.tile([P, WINDOW], F32)
+        nc.vector.tensor_copy(out=diff[:], in_=diff_i[:])
+        inside = keep.tile([P, WINDOW], F32)
+        nc.vector.tensor_scalar(out=inside[:], in0=diff[:], scalar1=0.0, scalar2=None, op0=ALU.is_ge)
+        nc.vector.scalar_tensor_tensor(
+            out=inside[:], in0=diff[:], scalar=float(BAND - 1), in1=inside[:], op0=ALU.is_le, op1=ALU.mult
+        )
+        band_mask = keep.tile([P, SEQ_TILES, WINDOW], F32)
+        for i in range(SEQ_TILES):
+            nc.vector.tensor_scalar(
+                out=band_mask[:, i, :], in0=inside[:], scalar1=1.0, scalar2=-MASKED, op0=ALU.subtract, op1=ALU.mult
+            )
+        nc.vector.memset(band_mask[:, 0, 0:HALO], MASKED)
+        nc.vector.memset(band_mask[:, SEQ_TILES - 1, WINDOW - HALO :], MASKED)
+        on_diag = keep.tile([P, WINDOW], F32)
+        nc.vector.tensor_scalar(out=on_diag[:], in0=diff[:], scalar1=0.0, scalar2=None, op0=ALU.is_equal)
+        turn = keep.tile([P, SLOTS], F32)
+        nc.vector.tensor_reduce(
+            out=turn[:], in_=on_diag[:].rearrange("p (a r) -> p r a", r=SLOTS), axis=AXIS_X, op=ALU.add
+        )
+        place_i = keep.tile([P, RUN], I32)
+        nc.gpsimd.iota(place_i[:], pattern=[[1, RUN]], base=0, channel_multiplier=RUN)
+        place_m = keep.tile([P, RUN], I32)
+        nc.vector.tensor_scalar(out=place_m[:], in0=place_i[:], scalar1=SEQ - 1, scalar2=None, op0=ALU.bitwise_and)
+        place = keep.tile([P, RUN], F32)
+        nc.vector.tensor_copy(out=place[:], in_=place_m[:])
+        edge = keep.tile([P, RUN, BAND], F32)
+        nc.vector.memset(edge[:], 0.0)
+        for j in range(HALO):
+            nc.vector.tensor_scalar(
+                out=edge[:, :, j], in0=place[:], scalar1=float(HALO - j), scalar2=MASKED, op0=ALU.is_lt, op1=ALU.mult
+            )
+            nc.vector.tensor_scalar(
+                out=edge[:, :, BAND - 1 - j], in0=place[:], scalar1=float(SEQ - 1 - HALO + j), scalar2=MASKED,
+                op0=ALU.is_gt, op1=ALU.mult,
             )
 
-        load_x(0)
+        def load_x_run(g):
+            steps = slice(g * GROUP, (g + 1) * GROUP)
+            nc.sync.dma_start(out=x_run[:, steps, :], in_=x_steps[:, steps, :])
+
+        def load_k_run(g):
+            nc.sync.dma_start(
+                out=k_ext[:, HALO + g * GROUP : HALO + (g + 1) * GROUP, :],
+                in_=k_steps[:, g * GROUP : (g + 1) * GROUP, :],
+            )
+
+        def load_x_band(n):
+            tiles = slice(2 * SEQ_TILES * n, 2 * SEQ_TILES * (n + 1))
+            nc.sync.dma_start(out=x_band[:, tiles, :], in_=x_tiles[:, tiles, :])
+
+        def load_k_band(n):
+            tiles = slice(2 * SEQ_TILES * n, 2 * SEQ_TILES * (n + 1))
+            nc.sync.dma_start(out=k_band[:, tiles, :], in_=k_tiles[:, tiles, :])
+
+        load_x_run(0)
         nc.sync.dma_start(out=w_words[:].bitcast(I32), in_=Wq_words[0].bitcast(I32))
         for quadrant in range(4):
             nc.sync.dma_start(
                 out=w_plane[32 * quadrant : 32 * quadrant + 4, :].bitcast(I32),
                 in_=Wq_scales[0, 4 * quadrant : 4 * quadrant + 4, :].bitcast(I32),
             )
-        nc.scalar.dma_start(out=k_ext[1:16, 0:HALO, :], in_=k_steps[0:15, STEPS - HALO :, :])
-        nc.scalar.dma_start(out=k_ext[16:P, 0:HALO, :], in_=k_steps[15 : P - 1, STEPS - HALO :, :])
-        nc.scalar.dma_start(
-            out=bias_rows[0:D_BLOCKS, :], in_=bq.rearrange("(c d) -> c d", c=D_BLOCKS)
-        )
-        nc.scalar.dma_start(out=k_ext[0:112, STEPS + HALO :, :], in_=k_steps[1:113, 0:HALO, :])
-        nc.scalar.dma_start(out=k_ext[112 : P - 1, STEPS + HALO :, :], in_=k_steps[113:P, 0:HALO, :])
-        load_x(1)
-        load_k(0)
-        load_k(1)
-        for m in range(2, GROUPS):
-            load_x(m)
-            load_k(m)
+        nc.scalar.dma_start(out=k_ext[:, 0:HALO, :], in_=k_before[:, 0:HALO, :])
+        nc.scalar.dma_start(out=bias_rows[0:D_BLOCKS, :], in_=bq.rearrange("(c d) -> c d", c=D_BLOCKS))
+        nc.scalar.dma_start(out=bias_pairs[0:2, :], in_=bq.rearrange("(u n) -> u n", u=2))
+        nc.scalar.dma_start(out=k_ext[0:112, RUN + HALO :, :], in_=k_after[0:112, 0:HALO, :])
+        nc.scalar.dma_start(out=k_ext[112 : P - 1, RUN + HALO :, :], in_=k_after[112 : P - 1, 0:HALO, :])
+        loads = []
+        for g in range(1, GROUPS):
+            loads.append((g * GROUP - X_LEAD, 0, load_x_run, g))
+        for g in range(GROUPS):
+            loads.append((g * GROUP - ROWS_LEAD, 1, load_k_run, g))
+        for n in range(BAND_SEQS // 2):
+            loads.append((BAND_START + 2 * BAND_PERIOD * n, 2, load_x_band, n))
+            loads.append((BAND_START + 2 * BAND_PERIOD * n + 1, 3, load_k_band, n))
+        for entry in sorted(loads, key=lambda item: (item[0], item[1])):
+            entry[2](entry[3])
 
-        x_words = x_all[:].rearrange("p t k -> p (t k)").bitcast(F32)
-        x_words = x_words.rearrange("p (t w) -> p t w", t=STEPS)
+        bias = {}
+
+        def prepare_bias():
+            bias_t = psum_t.tile([P, P], BF16, name="tp")
+            nc.tensor.transpose(bias_t[:], bias_rows[:], ident_bf[:])
+            bias_scaled = keep.tile([P, D_BLOCKS], F32)
+            nc.scalar.activation(out=bias_scaled[:], in_=bias_t[:, 0:D_BLOCKS], func=ACT.Copy, scale=INV_SQRT_D)
+            pair_t = psum_t.tile([P, P], F32, name="tp")
+            nc.tensor.transpose(pair_t[:], bias_pairs[:].bitcast(F32), ident[:])
+            bias_words = keep.tile([P, 2], F32)
+            nc.scalar.copy(out=bias_words[:], in_=pair_t[:, 0:2])
+            bias["scaled"] = bias_scaled
+            bias["cols"] = bias_words[:].bitcast(BF16)
+
+        def words_of(tile_ap, count):
+            flat = tile_ap.rearrange("p t k -> p (t k)").bitcast(F32)
+            return flat.rearrange("p (t w) -> p t w", t=count)
+
+        x_run_words = words_of(x_run[:], RUN)
+        x_band_words = words_of(x_band[:], BAND_TILES)
+        k_words = words_of(k_ext[:], ROWS)
+
+        def transpose_x_pair(words, first, dest):
+            xt = psum_t.tile([P, PAIR, 2, P], F32, name="tp")
+            for i in range(PAIR):
+                for u in range(2):
+                    nc.tensor.transpose(xt[:, i, u, :], words[:, first + i, u : D // 2 : 2], ident[:])
+            nc.scalar.copy(out=dest, in_=xt[:].rearrange("q t u p -> q t p u"))
+
         grouped_of = {}
         quantised_of = {}
 
-        def transpose_x_pair(first):
-            m = first // GROUP
+        def transpose_run_pair(first):
+            g = first // GROUP
             if first % GROUP == 0:
-                grouped_of[m] = quant.tile([P, GROUP * P * 4], BF16, align_bytes=64, name="grouped")
-            grouped_words = grouped_of[m][:].bitcast(F32).rearrange(
-                "q (t p u) -> q t p u", t=GROUP, u=2
-            )
-            xt = psum_x.tile([P, PAIR, 2, P], F32, name="xt")
-            for i in range(PAIR):
-                for u in range(2):
-                    nc.tensor.transpose(xt[:, i, u, :], x_words[:, first + i, u : D // 2 : 2], ident[:])
-            nc.scalar.copy(
-                out=grouped_words[:, first % GROUP : first % GROUP + PAIR, :, :],
-                in_=xt[:].rearrange("q t u p -> q t p u"),
-            )
+                grouped_of[g] = quant.tile([P, GROUP * P * 4], BF16, align_bytes=64, name="grouped")
+            grouped_words = grouped_of[g][:].bitcast(F32).rearrange("q (t p u) -> q t p u", t=GROUP, u=2)
+            transpose_x_pair(x_run_words, first, grouped_words[:, first % GROUP : first % GROUP + PAIR, :, :])
 
-        def quantise_group(m):
+        def quantise_group(g):
             codes = quant.tile([P, GROUP * P], U32, align_bytes=64, name="codes")
             scales = quant.tile([P, GROUP * P], U8, align_bytes=64, name="scales")
-            nc.vector.quantize_mx(
-                out=codes[:].bitcast(FP8X4), scales=scales[:], in_=grouped_of[m][:]
-            )
-            quantised_of[m] = (codes, scales)
+            nc.vector.quantize_mx(out=codes[:].bitcast(FP8X4), scales=scales[:], in_=grouped_of[g][:])
+            quantised_of[g] = (codes, scales)
 
         def project(t):
             codes, scales = quantised_of[t // GROUP]
@@ -159,7 +249,7 @@ def tile_crosssliceattention_pa_t_kernel(tc, x, Wq_words, Wq_scales, bq, k_proj,
 
         def scores_on_vector(t, q_ps):
             for j in range(BAND):
-                junk = junk_pool.tile([P, D], F32, name="junk")
+                junk = work.tile([P, D], F32, name="junk")
                 nc.vector.scalar_tensor_tensor(
                     out=junk[:],
                     in0=q_ps[:],
@@ -175,13 +265,11 @@ def tile_crosssliceattention_pa_t_kernel(tc, x, Wq_words, Wq_scales, bq, k_proj,
             nc.scalar.copy(out=q_sb[:], in_=q_ps[:])
             products = work.tile([P, BAND, D], F32, name="products")
             for j in range(BAND):
-                nc.gpsimd.tensor_tensor(
-                    out=products[:, j, :], in0=q_sb[:], in1=k_ext[:, t + j, :], op=ALU.mult
-                )
+                nc.gpsimd.tensor_tensor(out=products[:, j, :], in0=q_sb[:], in1=k_ext[:, t + j, :], op=ALU.mult)
             return products
 
-        def sum_on_scalar(t, products):
-            for j in range(BAND):
+        def sum_on_scalar(t, products, neighbours):
+            for j in neighbours:
                 nc.scalar.activation(
                     out=products[:, j, :],
                     in_=products[:, j, :],
@@ -190,96 +278,244 @@ def tile_crosssliceattention_pa_t_kernel(tc, x, Wq_words, Wq_scales, bq, k_proj,
                     accum_out=raw[:, t, j : j + 1],
                 )
 
-        def transpose_k_pair(first):
-            kt = psum_k.tile([P, PAIR, D_BLOCKS, P], BF16, name="kt")
+        def transpose_rows(first):
+            kw = psum_t.tile([P, PAIR, 2, P], F32, name="tp")
             for i in range(PAIR):
-                for c in range(D_BLOCKS):
-                    nc.tensor.transpose(kt[:, i, c, :], k_ext[:, first + i, c * P : (c + 1) * P], ident_bf[:])
-            kt_sb = work.tile([P, PAIR, D_BLOCKS, P], BF16, name="kt_sb")
-            nc.scalar.copy(out=kt_sb[:], in_=kt[:])
-            return kt_sb
+                for u in range(2):
+                    nc.tensor.transpose(kw[:, i, u, :], k_words[:, first + i, u * P : (u + 1) * P], ident[:])
+            kw_sb = rows_pool.tile([P, PAIR * 2 * P], F32, name="kw_sb")
+            nc.scalar.copy(out=kw_sb[:], in_=kw[:].rearrange("w i u p -> w (i u p)"))
+            return kw_sb
 
-        def bias_dot_pair(first, kt_sb):
+        def bias_dot_pair(first, kw_sb):
+            halves = kw_sb[:].bitcast(BF16).rearrange("w (i u p e) -> w i u p e", i=PAIR, u=2, e=2)
             for i in range(PAIR):
-                for c in range(D_BLOCKS):
+                for n in range(4):
                     nc.tensor.matmul(
                         out=bias_dot[:, first + i : first + i + 1],
-                        lhsT=kt_sb[:, i, c, :],
-                        rhs=bias_cols[:, c : c + 1],
+                        lhsT=halves[:, i, n // 2, :, n % 2],
+                        rhs=bias["cols"][:, n : n + 1],
+                        start=(n == 0),
+                        stop=(n == 3),
+                    )
+
+        band_grouped = {}
+        band_quantised = {}
+        query_cols = {}
+        band_scores_of = {}
+
+        def band_x(s):
+            grouped = quant.tile([P, SEQ * 4], BF16, align_bytes=64, name="grouped_b")
+            dest = grouped[:].bitcast(F32).rearrange("q (t p u) -> q t p u", t=SEQ_TILES, u=2)
+            transpose_x_pair(x_band_words, SEQ_TILES * s, dest)
+            band_grouped[s] = grouped
+
+        def band_k(s):
+            codes = quant.tile([P, SEQ], U32, align_bytes=64, name="codes_b")
+            scales = quant.tile([P, SEQ], U8, align_bytes=64, name="scales_b")
+            nc.vector.quantize_mx(out=codes[:].bitcast(FP8X4), scales=scales[:], in_=band_grouped[s][:])
+            band_quantised[s] = (codes, scales)
+            kt = psum_t.tile([P, SEQ_TILES, D_BLOCKS, P], BF16, name="tp")
+            for i in range(SEQ_TILES):
+                for c in range(D_BLOCKS):
+                    nc.tensor.transpose(kt[:, i, c, :], k_band[:, SEQ_TILES * s + i, c * P : (c + 1) * P], ident_bf[:])
+            cols = key_cols[s % len(key_cols)]
+            nc.scalar.copy(
+                out=cols[:, :, HALO : HALO + SEQ].rearrange("d c (i n) -> d i c n", i=SEQ_TILES), in_=kt[:]
+            )
+
+        def band_q(s, half):
+            codes, scales = band_quantised[s]
+            if half == 0:
+                query_cols[s] = work.tile([P, D_BLOCKS, SEQ], F32, name="q_cols")
+            qt = psum_c.tile([P, 2, SEQ], F32, name="qt")
+            for n in range(2):
+                c = 2 * half + n
+                nc.tensor.matmul_mx(
+                    out=qt[:, n, :],
+                    lhsT=w_words[:, 2 * P * c : 2 * P * (c + 1)].bitcast(FP4X4),
+                    lhsT_scale=w_plane[:, P * c : P * (c + 1)],
+                    rhs=codes[:].bitcast(FP8X4),
+                    rhs_scale=scales[:],
+                    start=True,
+                    stop=True,
+                )
+            for n in range(2):
+                c = 2 * half + n
+                nc.scalar.activation(
+                    out=query_cols[s][:, c, :],
+                    in_=qt[:, n, :],
+                    func=ACT.Identity,
+                    bias=bias["scaled"][:, c : c + 1],
+                    scale=INV_SQRT_D,
+                )
+
+        def band_q_first(s):
+            band_q(s, 0)
+
+        def band_q_second(s):
+            band_q(s, 1)
+
+        def band_multiply(s):
+            sc = psum_s.tile([P, SEQ_TILES, WINDOW], F32, name="sc")
+            cols = key_cols[s % len(key_cols)]
+            for i in range(SEQ_TILES):
+                for c in range(D_BLOCKS):
+                    nc.tensor.matmul(
+                        out=sc[:, i, :],
+                        lhsT=query_cols[s][:, c, i * P : (i + 1) * P],
+                        rhs=cols[:, c, i * P : i * P + WINDOW],
                         start=(c == 0),
                         stop=(c == D_BLOCKS - 1),
                     )
+            band_scores_of[s] = sc
 
-        for first in range(0, 2 * GROUP, PAIR):
-            transpose_x_pair(first)
-        quantise_group(0)
-        bias_t = psum_k.tile([P, PAIR, D_BLOCKS, P], BF16, name="kt")
-        nc.tensor.transpose(bias_t[:, 0, 0, :], bias_rows[:], ident_bf[:])
-        nc.scalar.copy(out=bias_cols[:], in_=bias_t[:, 0, 0, 0:D_BLOCKS])
-
-        waiting_rows = []
-        waiting_products = []
-
-        def bias_term_of_rows(first):
-            waiting_rows.append((first, transpose_k_pair(first)))
-            if len(waiting_rows) > 1:
-                bias_dot_pair(*waiting_rows.pop(0))
-
-        for m in range(GROUPS):
-            if m + 1 < GROUPS:
-                quantise_group(m + 1)
-            for t in range(m * GROUP, (m + 1) * GROUP):
-                q_ps = project(t)
-                on_gpsimd = t % GPSIMD_EVERY == 1
-                if on_gpsimd:
-                    waiting_products.append((t, multiply_on_gpsimd(t, q_ps)))
-                    if len(waiting_products) > 1:
-                        sum_on_scalar(*waiting_products.pop(0))
-                if t % PAIR == 1:
-                    bias_term_of_rows(t - 1)
-                elif t + 2 * GROUP < STEPS:
-                    transpose_x_pair(t + 2 * GROUP)
-                elif t + 2 * GROUP < ROWS:
-                    bias_term_of_rows(t + 2 * GROUP)
-                if not on_gpsimd:
-                    scores_on_vector(t, q_ps)
-        bias_dot_pair(*waiting_rows.pop(0))
-        sum_on_scalar(*waiting_products.pop(0))
-
-        scores = keep.tile([P, STEPS, BAND], F32)
-        for j in range(BAND):
-            nc.vector.scalar_tensor_tensor(
-                out=scores[:, :, j],
-                in0=bias_dot[:, j : j + STEPS],
-                scalar=INV_SQRT_D,
-                in1=raw[:, :, j],
-                op0=ALU.mult,
-                op1=ALU.add,
+        def band_extract(s):
+            masked = work.tile([P, SEQ_TILES, WINDOW], F32, name="masked")
+            nc.vector.tensor_tensor(out=masked[:], in0=band_scores_of[s][:], in1=band_mask[:], op=ALU.add)
+            nc.vector.tensor_reduce(
+                out=slots[:, SEQ_TILES * s : SEQ_TILES * (s + 1), :],
+                in_=masked[:].rearrange("p i (a r) -> p i r a", r=SLOTS),
+                axis=AXIS_X,
+                op=ALU.max,
             )
-        for i in range(HALO):
-            low = scores[:, i, 0 : HALO - i]
-            nc.vector.tensor_scalar_add(out=low, in0=low, scalar1=neg[:, 0:1])
-            high = scores[:, STEPS - 1 - i, BAND - HALO + i : BAND]
-            nc.vector.tensor_scalar_add(
-                out=high, in0=high, scalar1=neg[:, PARTS_PER_SEQ - 1 : PARTS_PER_SEQ]
+
+        band_stages = [band_x, band_k, band_q_first, band_q_second, band_multiply, band_extract]
+
+        def exponentials(scores, count, label):
+            top = keep.tile([P, count], F32, name="top_" + label)
+            nc.vector.tensor_reduce(out=top[:], in_=scores[:], axis=AXIS_X, op=ALU.max)
+            weights = keep.tile([P, count, BAND], F32, name="weights_" + label)
+            nc.vector.tensor_tensor(
+                out=weights[:], in0=scores[:], in1=top[:].unsqueeze(2).to_broadcast([P, count, BAND]), op=ALU.subtract
             )
-        top = keep.tile([P, STEPS], F32)
-        nc.vector.tensor_reduce(out=top[:], in_=scores[:], axis=AXIS_X, op=ALU.max)
-        weights = keep.tile([P, STEPS, BAND], F32)
+            nc.scalar.activation(out=weights[:], in_=weights[:], func=ACT.Exp)
+            return weights
+
+        def inverse_sums(weights, count, label):
+            total = keep.tile([P, count], F32, name="total_" + label)
+            nc.vector.tensor_reduce(out=total[:], in_=weights[:], axis=AXIS_X, op=ALU.add)
+            nc.vector.reciprocal(out=total[:], in_=total[:])
+            return total
+
+        band_end = {}
+
+        def band_end_scores():
+            twice = keep.tile([P, BAND_TILES, 2, SLOTS], F32)
+            nc.vector.tensor_copy(out=twice[:], in_=slots[:].unsqueeze(2).to_broadcast([P, BAND_TILES, 2, SLOTS]))
+            wrapped = twice[:].rearrange("p i w r -> p i (w r)")
+            band_sc = keep.tile([P, BAND_TILES, BAND], F32)
+            nc.vector.tensor_scalar_mul(out=band_sc[:], in0=wrapped[:, :, 0:BAND], scalar1=turn[:, 0:1])
+            for r in range(1, SLOTS):
+                nc.vector.scalar_tensor_tensor(
+                    out=band_sc[:],
+                    in0=wrapped[:, :, r : r + BAND],
+                    scalar=turn[:, r : r + 1],
+                    in1=band_sc[:],
+                    op0=ALU.mult,
+                    op1=ALU.add,
+                )
+            band_end["weights"] = exponentials(band_sc, BAND_TILES, "band")
+
+        def band_end_normalise():
+            weights = band_end["weights"]
+            total = inverse_sums(weights, BAND_TILES, "band")
+            spread = keep.tile([P, 2, 2, HALF_COLS], F32)
+            nc.vector.memset(spread[:], 0.0)
+            for e in range(2):
+                nc.vector.tensor_tensor(
+                    out=spread[:, :, e, 0 : HALF_TILES * BAND].rearrange("p h (t j) -> p h t j", j=BAND),
+                    in0=weights[:].rearrange("p (h t) j -> p h t j", h=2),
+                    in1=total[:].rearrange("p (h t) -> p h t", h=2).unsqueeze(3).to_broadcast([P, 2, HALF_TILES, BAND]),
+                    op=ALU.mult,
+                )
+            t1 = psum_t.tile([P, 2, P], F32, name="tp")
+            for h in range(2):
+                nc.tensor.transpose(t1[:, h, :], spread[:, h, :, :].rearrange("p e m -> p (e m)"), ident[:])
+            band_end["t1"] = t1
+
+        def band_end_pair():
+            t1 = band_end["t1"]
+            paired = keep.tile([P, P], F32)
+            for e in range(2):
+                rows = slice(HALF_COLS * e, HALF_COLS * (e + 1))
+                nc.scalar.copy(out=paired[rows, :].rearrange("m (h u) -> m h u", h=2), in_=t1[rows, :, e:P:2])
+            t2 = psum_t.tile([P, P], F32, name="tp")
+            nc.tensor.transpose(t2[:], paired[:], ident[:])
+            band_end["t2"] = t2
+
+        def band_end_store():
+            t2 = band_end["t2"]
+            band_out = keep.tile([P, HALF_TILES, 2, BAND], F32)
+            nc.scalar.copy(
+                out=band_out[:],
+                in_=t2[:].rearrange("p (e m) -> p e m", e=2)[:, :, 0 : HALF_TILES * BAND].rearrange(
+                    "p e (t j) -> p t e j", j=BAND
+                ),
+            )
+            for h in range(2):
+                tokens = slice(HALF_TILES * P * h, HALF_TILES * P * (h + 1))
+                nc.sync.dma_start(
+                    out=out_flat[tokens, :].rearrange("(t u e) j -> u t (e j)", t=HALF_TILES, e=2),
+                    in_=band_out[HALF_COLS * h : HALF_COLS * (h + 1), :, :, :].rearrange("p t e j -> p t (e j)"),
+                )
+
+        band_end_phases = [band_end_scores, band_end_normalise, band_end_pair, band_end_store]
+        BAND_END_TICK = BAND_START + BAND_PERIOD * (BAND_SEQS - 1) + len(band_stages)
+
+        products_of = {}
+        rows_of = {}
+        addend = keep.tile([P, RUN, BAND], F32)
+
+        for tick in range(FIRST_TICK, LAST_TICK):
+            in_run = 0 <= tick < RUN
+            on_gpsimd = in_run and tick % GPSIMD_EVERY == 1
+            q_ps = None
+            if in_run:
+                q_ps = project(tick)
+            if on_gpsimd:
+                products_of[tick] = multiply_on_gpsimd(tick, q_ps)
+            for lag, neighbours in SUM_PLAN:
+                if tick - lag in products_of:
+                    sum_on_scalar(tick - lag, products_of[tick - lag], neighbours)
+            if tick - 2 in rows_of:
+                bias_dot_pair(*rows_of[tick - 2])
+            if tick == FIRST_TICK + 3:
+                prepare_bias()
+            if tick % 2 == 0:
+                first = tick + X_LEAD
+                if first < RUN:
+                    transpose_run_pair(first)
+                elif first < ROWS:
+                    rows_of[tick] = (first, transpose_rows(first))
+            elif 0 <= tick + ROWS_LEAD < RUN:
+                rows_of[tick] = (tick + ROWS_LEAD, transpose_rows(tick + ROWS_LEAD))
+            for depth in reversed(range(len(band_stages))):
+                s, rest = divmod(tick - depth - BAND_START, BAND_PERIOD)
+                if rest == 0 and 0 <= s < BAND_SEQS:
+                    band_stages[depth](s)
+            if 0 <= tick - BAND_END_TICK < len(band_end_phases):
+                band_end_phases[tick - BAND_END_TICK]()
+            if tick % GROUP == 0 and 0 <= tick // GROUP + 1 < GROUPS:
+                quantise_group(tick // GROUP + 1)
+            if tick == RUN - 2:
+                for j in range(BAND):
+                    nc.vector.scalar_tensor_tensor(
+                        out=addend[:, :, j],
+                        in0=bias_dot[:, j : j + RUN],
+                        scalar=INV_SQRT_D,
+                        in1=edge[:, :, j],
+                        op0=ALU.mult,
+                        op1=ALU.add,
+                    )
+            if in_run and not on_gpsimd:
+                scores_on_vector(tick, q_ps)
+
+        scores = keep.tile([P, RUN, BAND], F32)
+        nc.vector.tensor_tensor(out=scores[:], in0=raw[:, :, 0:BAND], in1=addend[:], op=ALU.add)
+        weights = exponentials(scores, RUN, "run")
+        total = inverse_sums(weights, RUN, "run")
         nc.vector.tensor_tensor(
-            out=weights[:],
-            in0=scores[:],
-            in1=top[:].unsqueeze(2).to_broadcast([P, STEPS, BAND]),
-            op=ALU.subtract,
+            out=weights[:], in0=weights[:], in1=total[:].unsqueeze(2).to_broadcast([P, RUN, BAND]), op=ALU.mult
         )
-        nc.scalar.activation(out=weights[:], in_=weights[:], func=ACT.Exp)
-        total = keep.tile([P, STEPS], F32)
-        nc.vector.tensor_reduce(out=total[:], in_=weights[:], axis=AXIS_X, op=ALU.add)
-        nc.vector.reciprocal(out=total[:], in_=total[:])
-        nc.vector.tensor_tensor(
-            out=weights[:],
-            in0=weights[:],
-            in1=total[:].unsqueeze(2).to_broadcast([P, STEPS, BAND]),
-            op=ALU.mult,
-        )
-        nc.sync.dma_start(out=out_rows, in_=weights[:].rearrange("p t j -> p (t j)"))
+        nc.sync.dma_start(out=out_run, in_=weights[:].rearrange("p t j -> p (t j)"))

@@ -33,8 +33,8 @@ WINDOW = P + 2 * HALO
 SLOTS = BAND + 1
 HALF_TILES = BAND_TILES // 2
 HALF_COLS = P // 2
-BAND_PERIOD = 3
-BAND_START = -4
+BAND_NUM = 8
+BAND_DEN = 3
 
 RUN = (TOKENS - BAND_TOKENS) // P
 ROWS = RUN + 2 * HALO
@@ -43,11 +43,12 @@ GROUPS = RUN // GROUP
 PAIR = 2
 SCORE_PAD = 8
 X_LEAD = 2 * GROUP
-ROWS_LEAD = 3
 GPSIMD_EVERY = 3
 SUM_PLAN = ((2, (0, 1)), (3, (2, 3)), (4, (4,)))
-FIRST_TICK = -X_LEAD
+FIRST_TICK = -2
 LAST_TICK = RUN + 2
+ROWS_SINGLE = 16
+BAND_X_ON_VECTOR = False
 
 FLOPS = 2 * TOKENS * D * D + 2 * TOKENS * BAND * D
 
@@ -72,7 +73,7 @@ def tile_crosssliceattention_pa_t_kernel(tc, x, Wq_words, Wq_scales, bq, k_proj,
         rows_pool = stack.enter_context(tc.tile_pool(name="rows_pool", bufs=3))
         work = stack.enter_context(tc.tile_pool(name="work", bufs=2))
         psum_t = stack.enter_context(tc.psum_pool(name="psum_t", bufs=2))
-        psum_q = stack.enter_context(tc.psum_pool(name="psum_q", bufs=3))
+        psum_q = stack.enter_context(tc.psum_pool(name="psum_q", bufs=2))
         psum_c = stack.enter_context(tc.psum_pool(name="psum_c", bufs=1))
         psum_s = stack.enter_context(tc.psum_pool(name="psum_s", bufs=1))
         psum_b = stack.enter_context(tc.psum_pool(name="psum_b", bufs=1))
@@ -146,6 +147,15 @@ def tile_crosssliceattention_pa_t_kernel(tc, x, Wq_words, Wq_scales, bq, k_proj,
                 op0=ALU.is_gt, op1=ALU.mult,
             )
 
+        def x_tick(first):
+            return max(first - X_LEAD, first // 2 + FIRST_TICK)
+
+        def band_tick(s):
+            return (s * BAND_NUM) // BAND_DEN
+
+        def rows_tick(n):
+            return 2 * n + 1 if n < ROWS_SINGLE else 2 * ROWS_SINGLE + (n - ROWS_SINGLE)
+
         def load_x_run(g):
             steps = slice(g * GROUP, (g + 1) * GROUP)
             nc.sync.dma_start(out=x_run[:, steps, :], in_=x_steps[:, steps, :])
@@ -178,12 +188,12 @@ def tile_crosssliceattention_pa_t_kernel(tc, x, Wq_words, Wq_scales, bq, k_proj,
         nc.scalar.dma_start(out=k_ext[112 : P - 1, RUN + HALO :, :], in_=k_after[112 : P - 1, 0:HALO, :])
         loads = []
         for g in range(1, GROUPS):
-            loads.append((g * GROUP - X_LEAD, 0, load_x_run, g))
+            loads.append((x_tick(g * GROUP), 0, load_x_run, g))
         for g in range(GROUPS):
-            loads.append((g * GROUP - ROWS_LEAD, 1, load_k_run, g))
+            loads.append((g * GROUP - HALO - 1, 1, load_k_run, g))
         for n in range(BAND_SEQS // 2):
-            loads.append((BAND_START + 2 * BAND_PERIOD * n, 2, load_x_band, n))
-            loads.append((BAND_START + 2 * BAND_PERIOD * n + 1, 3, load_k_band, n))
+            loads.append((band_tick(2 * n), 2, load_x_band, n))
+            loads.append((band_tick(2 * n) + 1, 3, load_k_band, n))
         for entry in sorted(loads, key=lambda item: (item[0], item[1])):
             entry[2](entry[3])
 
@@ -209,12 +219,15 @@ def tile_crosssliceattention_pa_t_kernel(tc, x, Wq_words, Wq_scales, bq, k_proj,
         x_band_words = words_of(x_band[:], BAND_TILES)
         k_words = words_of(k_ext[:], ROWS)
 
-        def transpose_x_pair(words, first, dest):
+        def transpose_x_pair(words, first, dest, on_vector=False):
             xt = psum_t.tile([P, PAIR, 2, P], F32, name="tp")
             for i in range(PAIR):
                 for u in range(2):
                     nc.tensor.transpose(xt[:, i, u, :], words[:, first + i, u : D // 2 : 2], ident[:])
-            nc.scalar.copy(out=dest, in_=xt[:].rearrange("q t u p -> q t p u"))
+            if on_vector:
+                nc.vector.tensor_copy(out=dest, in_=xt[:].rearrange("q t u p -> q t p u"))
+            else:
+                nc.scalar.copy(out=dest, in_=xt[:].rearrange("q t u p -> q t p u"))
 
         grouped_of = {}
         quantised_of = {}
@@ -307,7 +320,7 @@ def tile_crosssliceattention_pa_t_kernel(tc, x, Wq_words, Wq_scales, bq, k_proj,
         def band_x(s):
             grouped = quant.tile([P, SEQ * 4], BF16, align_bytes=64, name="grouped_b")
             dest = grouped[:].bitcast(F32).rearrange("q (t p u) -> q t p u", t=SEQ_TILES, u=2)
-            transpose_x_pair(x_band_words, SEQ_TILES * s, dest)
+            transpose_x_pair(x_band_words, SEQ_TILES * s, dest, BAND_X_ON_VECTOR)
             band_grouped[s] = grouped
 
         def band_k(s):
@@ -356,31 +369,35 @@ def tile_crosssliceattention_pa_t_kernel(tc, x, Wq_words, Wq_scales, bq, k_proj,
         def band_q_second(s):
             band_q(s, 1)
 
-        def band_multiply(s):
-            sc = psum_s.tile([P, SEQ_TILES, WINDOW], F32, name="sc")
+        sc_0 = psum_s.tile([P, SEQ_TILES, WINDOW], F32)
+        sc_1 = psum_s.tile([P, SEQ_TILES, WINDOW], F32)
+        sc_of = [sc_0, sc_1]
+        masked_of = {}
+
+        def band_multiply(s, parts):
             cols = key_cols[s % len(key_cols)]
-            for i in range(SEQ_TILES):
-                for c in range(D_BLOCKS):
-                    nc.tensor.matmul(
-                        out=sc[:, i, :],
-                        lhsT=query_cols[s][:, c, i * P : (i + 1) * P],
-                        rhs=cols[:, c, i * P : i * P + WINDOW],
-                        start=(c == 0),
-                        stop=(c == D_BLOCKS - 1),
-                    )
-            band_scores_of[s] = sc
+            for part in parts:
+                i, c = divmod(part, D_BLOCKS)
+                nc.tensor.matmul(
+                    out=sc_of[s % 2][:, i, :],
+                    lhsT=query_cols[s][:, c, i * P : (i + 1) * P],
+                    rhs=cols[:, c, i * P : i * P + WINDOW],
+                    start=(c == 0),
+                    stop=(c == D_BLOCKS - 1),
+                )
+
+        def band_mask_tile(s, i):
+            if i == 0:
+                masked_of[s] = work.tile([P, SEQ_TILES, WINDOW], F32, name="masked")
+            nc.vector.tensor_tensor(out=masked_of[s][:, i, :], in0=sc_of[s % 2][:, i, :], in1=band_mask[:, i, :], op=ALU.add)
 
         def band_extract(s):
-            masked = work.tile([P, SEQ_TILES, WINDOW], F32, name="masked")
-            nc.vector.tensor_tensor(out=masked[:], in0=band_scores_of[s][:], in1=band_mask[:], op=ALU.add)
             nc.vector.tensor_reduce(
                 out=slots[:, SEQ_TILES * s : SEQ_TILES * (s + 1), :],
-                in_=masked[:].rearrange("p i (a r) -> p i r a", r=SLOTS),
+                in_=masked_of[s][:].rearrange("p i (a r) -> p i r a", r=SLOTS),
                 axis=AXIS_X,
                 op=ALU.max,
             )
-
-        band_stages = [band_x, band_k, band_q_first, band_q_second, band_multiply, band_extract]
 
         def exponentials(scores, count, label):
             top = keep.tile([P, count], F32, name="top_" + label)
@@ -461,44 +478,81 @@ def tile_crosssliceattention_pa_t_kernel(tc, x, Wq_words, Wq_scales, bq, k_proj,
                 )
 
         band_end_phases = [band_end_scores, band_end_normalise, band_end_pair, band_end_store]
-        BAND_END_TICK = BAND_START + BAND_PERIOD * (BAND_SEQS - 1) + len(band_stages)
+        BAND_END_TICK = band_tick(BAND_SEQS - 1) + 9
 
         products_of = {}
         rows_of = {}
         addend = keep.tile([P, RUN, BAND], F32)
+        x_at = {}
+        quant_at = {}
+        rows_at = {}
+        band_at = {}
+        for first in range(0, RUN, PAIR):
+            x_at[x_tick(first)] = first
+        for g in range(GROUPS):
+            quant_at[max(g * GROUP - GROUP, x_tick(g * GROUP + PAIR))] = g
+        for n in range(ROWS // PAIR):
+            rows_at[rows_tick(n)] = PAIR * n
+        for s in range(BAND_SEQS):
+            for depth in range(9):
+                band_at.setdefault(band_tick(s) + depth, []).append((depth, s))
 
         for tick in range(FIRST_TICK, LAST_TICK):
             in_run = 0 <= tick < RUN
             on_gpsimd = in_run and tick % GPSIMD_EVERY == 1
+            band_now = sorted(band_at.get(tick, []), reverse=True)
             q_ps = None
             if in_run:
                 q_ps = project(tick)
             if on_gpsimd:
                 products_of[tick] = multiply_on_gpsimd(tick, q_ps)
+            for depth, s in band_now:
+                if depth == 2:
+                    band_q(s, 0)
+                if depth == 3:
+                    band_q(s, 1)
             for lag, neighbours in SUM_PLAN:
                 if tick - lag in products_of:
                     sum_on_scalar(tick - lag, products_of[tick - lag], neighbours)
+            for depth, s in band_now:
+                if depth == 4:
+                    band_multiply(s, (0, 1))
+                if depth == 5:
+                    band_multiply(s, (3, 4))
+                if depth == 6:
+                    band_multiply(s, (6,))
             if tick - 2 in rows_of:
                 bias_dot_pair(*rows_of[tick - 2])
-            if tick == FIRST_TICK + 3:
+            if tick == 0:
                 prepare_bias()
-            if tick % 2 == 0:
-                first = tick + X_LEAD
-                if first < RUN:
-                    transpose_run_pair(first)
-                elif first < ROWS:
-                    rows_of[tick] = (first, transpose_rows(first))
-            elif 0 <= tick + ROWS_LEAD < RUN:
-                rows_of[tick] = (tick + ROWS_LEAD, transpose_rows(tick + ROWS_LEAD))
-            for depth in reversed(range(len(band_stages))):
-                s, rest = divmod(tick - depth - BAND_START, BAND_PERIOD)
-                if rest == 0 and 0 <= s < BAND_SEQS:
-                    band_stages[depth](s)
+            if tick in x_at:
+                transpose_run_pair(x_at[tick])
+            if tick in rows_at:
+                rows_of[tick] = (rows_at[tick], transpose_rows(rows_at[tick]))
+            for depth, s in band_now:
+                if depth == 0:
+                    band_x(s)
+            for depth, s in band_now:
+                if depth == 4:
+                    band_multiply(s, (2,))
+                if depth == 5:
+                    band_multiply(s, (5,))
+                if depth == 6:
+                    band_multiply(s, (7,))
+            for depth, s in band_now:
+                if depth == 1:
+                    band_k(s)
+            for depth, s in band_now:
+                if depth == 7:
+                    band_mask_tile(s, 0)
+                if depth == 8:
+                    band_mask_tile(s, 1)
+                    band_extract(s)
             if 0 <= tick - BAND_END_TICK < len(band_end_phases):
                 band_end_phases[tick - BAND_END_TICK]()
-            if tick % GROUP == 0 and 0 <= tick // GROUP + 1 < GROUPS:
-                quantise_group(tick // GROUP + 1)
-            if tick == RUN - 2:
+            if tick in quant_at:
+                quantise_group(quant_at[tick])
+            if tick == RUN - 1:
                 for j in range(BAND):
                     nc.vector.scalar_tensor_tensor(
                         out=addend[:, :, j],

@@ -44,9 +44,9 @@ PAIR = 2
 SCORE_PAD = 8
 X_LEAD = 2 * GROUP
 GPSIMD_EVERY = 3
-SUM_PLAN = ((2, (0, 1)), (3, (2, 3)), (4, (4,)))
+SUM_PLAN = ((3, (0, 1)), (4, (2, 3)), (5, (4,)))
 FIRST_TICK = -2
-LAST_TICK = RUN + 2
+LAST_TICK = RUN + 3
 ROWS_SINGLE = 16
 BAND_X_ON_VECTOR = False
 
@@ -93,7 +93,8 @@ def tile_crosssliceattention_pa_t_kernel(tc, x, Wq_words, Wq_scales, bq, k_proj,
         bias_dot = psum_b.tile([P, ROWS], F32)
         key_cols_0 = keep.tile([P, D_BLOCKS, SEQ + 2 * HALO], F32)
         key_cols_1 = keep.tile([P, D_BLOCKS, SEQ + 2 * HALO], F32)
-        key_cols = [key_cols_0, key_cols_1]
+        key_cols_2 = keep.tile([P, D_BLOCKS, SEQ + 2 * HALO], F32)
+        key_cols = [key_cols_0, key_cols_1, key_cols_2]
 
         nc.vector.memset(w_plane[:].bitcast(I32), 0)
         nc.vector.memset(k_ext[:, RUN + HALO :, :], 0.0)
@@ -273,10 +274,15 @@ def tile_crosssliceattention_pa_t_kernel(tc, x, Wq_words, Wq_scales, bq, k_proj,
                     accum_out=raw[:, t, j : j + 1],
                 )
 
-        def multiply_on_gpsimd(t, q_ps):
+        def copy_for_gpsimd(q_ps):
             q_sb = work.tile([P, D], F32, name="q_sb")
             nc.scalar.copy(out=q_sb[:], in_=q_ps[:])
+            return q_sb
+
+        def multiply_on_gpsimd(t, q_sb, gate):
             products = work.tile([P, BAND, D], F32, name="products")
+            if gate:
+                nc.vector.memset(products[:, 0, 0:1], 0.0)
             for j in range(BAND):
                 nc.gpsimd.tensor_tensor(out=products[:, j, :], in0=q_sb[:], in1=k_ext[:, t + j, :], op=ALU.mult)
             return products
@@ -323,11 +329,13 @@ def tile_crosssliceattention_pa_t_kernel(tc, x, Wq_words, Wq_scales, bq, k_proj,
             transpose_x_pair(x_band_words, SEQ_TILES * s, dest, BAND_X_ON_VECTOR)
             band_grouped[s] = grouped
 
-        def band_k(s):
+        def band_quantise(s):
             codes = quant.tile([P, SEQ], U32, align_bytes=64, name="codes_b")
             scales = quant.tile([P, SEQ], U8, align_bytes=64, name="scales_b")
             nc.vector.quantize_mx(out=codes[:].bitcast(FP8X4), scales=scales[:], in_=band_grouped[s][:])
             band_quantised[s] = (codes, scales)
+
+        def band_k(s):
             kt = psum_t.tile([P, SEQ_TILES, D_BLOCKS, P], BF16, name="tp")
             for i in range(SEQ_TILES):
                 for c in range(D_BLOCKS):
@@ -386,12 +394,9 @@ def tile_crosssliceattention_pa_t_kernel(tc, x, Wq_words, Wq_scales, bq, k_proj,
                     stop=(c == D_BLOCKS - 1),
                 )
 
-        def band_mask_tile(s, i):
-            if i == 0:
-                masked_of[s] = work.tile([P, SEQ_TILES, WINDOW], F32, name="masked")
-            nc.vector.tensor_tensor(out=masked_of[s][:, i, :], in0=sc_of[s % 2][:, i, :], in1=band_mask[:, i, :], op=ALU.add)
-
         def band_extract(s):
+            masked_of[s] = work.tile([P, SEQ_TILES, WINDOW], F32, name="masked")
+            nc.vector.tensor_tensor(out=masked_of[s][:], in0=sc_of[s % 2][:], in1=band_mask[:], op=ALU.add)
             nc.vector.tensor_reduce(
                 out=slots[:, SEQ_TILES * s : SEQ_TILES * (s + 1), :],
                 in_=masked_of[s][:].rearrange("p i (a r) -> p i r a", r=SLOTS),
@@ -478,7 +483,14 @@ def tile_crosssliceattention_pa_t_kernel(tc, x, Wq_words, Wq_scales, bq, k_proj,
                 )
 
         band_end_phases = [band_end_scores, band_end_normalise, band_end_pair, band_end_store]
-        BAND_END_TICK = band_tick(BAND_SEQS - 1) + 9
+
+        def is_gpsimd_tick(tick):
+            return 0 <= tick < RUN and tick % GPSIMD_EVERY == 1
+
+        def next_gpsimd_tick(tick):
+            while not is_gpsimd_tick(tick):
+                tick += 1
+            return tick
 
         products_of = {}
         rows_of = {}
@@ -490,37 +502,47 @@ def tile_crosssliceattention_pa_t_kernel(tc, x, Wq_words, Wq_scales, bq, k_proj,
         for first in range(0, RUN, PAIR):
             x_at[x_tick(first)] = first
         for g in range(GROUPS):
-            quant_at[max(g * GROUP - GROUP, x_tick(g * GROUP + PAIR))] = g
+            last_pair = x_tick(g * GROUP + PAIR)
+            quant_at.setdefault(last_pair if g == 0 else next_gpsimd_tick(last_pair), []).append(g)
         for n in range(ROWS // PAIR):
             rows_at[rows_tick(n)] = PAIR * n
+        project_tick = 0
         for s in range(BAND_SEQS):
-            for depth in range(9):
-                band_at.setdefault(band_tick(s) + depth, []).append((depth, s))
+            quantise_tick = next_gpsimd_tick(band_tick(s) + 1)
+            project_tick = max(quantise_tick + 1, project_tick + 2)
+            band_at.setdefault(band_tick(s), []).append(("x", s))
+            band_at.setdefault(quantise_tick, []).append(("quantise", s))
+            band_at.setdefault(project_tick - 1, []).append(("k", s))
+            for depth in range(6):
+                band_at.setdefault(project_tick + depth, []).append((depth, s))
+        BAND_END_TICK = project_tick + 6
 
         for tick in range(FIRST_TICK, LAST_TICK):
             in_run = 0 <= tick < RUN
-            on_gpsimd = in_run and tick % GPSIMD_EVERY == 1
-            band_now = sorted(band_at.get(tick, []), reverse=True)
+            on_gpsimd = is_gpsimd_tick(tick)
+            band_now = band_at.get(tick, [])
             q_ps = None
+            q_sb = None
             if in_run:
                 q_ps = project(tick)
             if on_gpsimd:
-                products_of[tick] = multiply_on_gpsimd(tick, q_ps)
-            for depth, s in band_now:
-                if depth == 2:
+                q_sb = copy_for_gpsimd(q_ps)
+            for what, s in band_now:
+                if what == 4:
+                    band_multiply(s, (6, 7))
+            for what, s in band_now:
+                if what == 0:
                     band_q(s, 0)
-                if depth == 3:
+                if what == 1:
                     band_q(s, 1)
             for lag, neighbours in SUM_PLAN:
                 if tick - lag in products_of:
                     sum_on_scalar(tick - lag, products_of[tick - lag], neighbours)
-            for depth, s in band_now:
-                if depth == 4:
+            for what, s in band_now:
+                if what == 2:
                     band_multiply(s, (0, 1))
-                if depth == 5:
+                if what == 3:
                     band_multiply(s, (3, 4))
-                if depth == 6:
-                    band_multiply(s, (6,))
             if tick - 2 in rows_of:
                 bias_dot_pair(*rows_of[tick - 2])
             if tick == 0:
@@ -529,29 +551,32 @@ def tile_crosssliceattention_pa_t_kernel(tc, x, Wq_words, Wq_scales, bq, k_proj,
                 transpose_run_pair(x_at[tick])
             if tick in rows_at:
                 rows_of[tick] = (rows_at[tick], transpose_rows(rows_at[tick]))
-            for depth, s in band_now:
-                if depth == 0:
+            for what, s in band_now:
+                if what == "x":
                     band_x(s)
-            for depth, s in band_now:
-                if depth == 4:
+            for what, s in band_now:
+                if what == 2:
                     band_multiply(s, (2,))
-                if depth == 5:
+                if what == 3:
                     band_multiply(s, (5,))
-                if depth == 6:
-                    band_multiply(s, (7,))
-            for depth, s in band_now:
-                if depth == 1:
+            for what, s in band_now:
+                if what == "k":
                     band_k(s)
-            for depth, s in band_now:
-                if depth == 7:
-                    band_mask_tile(s, 0)
-                if depth == 8:
-                    band_mask_tile(s, 1)
+            for what, s in band_now:
+                if what == 5:
                     band_extract(s)
             if 0 <= tick - BAND_END_TICK < len(band_end_phases):
                 band_end_phases[tick - BAND_END_TICK]()
-            if tick in quant_at:
-                quantise_group(quant_at[tick])
+            gate = False
+            for g in quant_at.get(tick, []):
+                quantise_group(g)
+                gate = True
+            for what, s in band_now:
+                if what == "quantise":
+                    band_quantise(s)
+                    gate = True
+            if on_gpsimd:
+                products_of[tick] = multiply_on_gpsimd(tick, q_sb, gate)
             if tick == RUN - 1:
                 for j in range(BAND):
                     nc.vector.scalar_tensor_tensor(

@@ -283,8 +283,13 @@ def tile_crosssliceattention_pa_t_kernel(tc, x, Wq_words, Wq_scales, bq, k_proj,
             products = work.tile([P, BAND, D], F32, name="products")
             if gate:
                 nc.vector.memset(products[:, 0, 0:1], 0.0)
-            for j in range(BAND):
-                nc.gpsimd.tensor_tensor(out=products[:, j, :], in0=q_sb[:], in1=k_ext[:, t + j, :], op=ALU.mult)
+            for low, high in ((0, 3), (3, BAND)):
+                nc.gpsimd.tensor_tensor(
+                    out=products[:, low:high, :],
+                    in0=q_sb[:].unsqueeze(1).to_broadcast([P, high - low, D]),
+                    in1=k_ext[:, t + low : t + high, :],
+                    op=ALU.mult,
+                )
             return products
 
         def sum_on_scalar(t, products, neighbours):

@@ -72,9 +72,8 @@ def tile_crosssliceattention_pa_t_kernel(tc, x, Wq_words, Wq_scales, bq, k_proj,
         quant = stack.enter_context(tc.tile_pool(name="quant", bufs=3))
         rows_pool = stack.enter_context(tc.tile_pool(name="rows_pool", bufs=3))
         work = stack.enter_context(tc.tile_pool(name="work", bufs=2))
-        psum_t = stack.enter_context(tc.psum_pool(name="psum_t", bufs=2))
+        psum_t = stack.enter_context(tc.psum_pool(name="psum_t", bufs=3))
         psum_q = stack.enter_context(tc.psum_pool(name="psum_q", bufs=2))
-        psum_c = stack.enter_context(tc.psum_pool(name="psum_c", bufs=1))
         psum_s = stack.enter_context(tc.psum_pool(name="psum_s", bufs=1))
         psum_b = stack.enter_context(tc.psum_pool(name="psum_b", bufs=1))
 
@@ -175,13 +174,14 @@ def tile_crosssliceattention_pa_t_kernel(tc, x, Wq_words, Wq_scales, bq, k_proj,
             tiles = slice(2 * SEQ_TILES * n, 2 * SEQ_TILES * (n + 1))
             nc.sync.dma_start(out=k_band[:, tiles, :], in_=k_tiles[:, tiles, :])
 
-        load_x_run(0)
+        nc.sync.dma_start(out=x_run[:, 0:PAIR, :], in_=x_steps[:, 0:PAIR, :])
         nc.sync.dma_start(out=w_words[:].bitcast(I32), in_=Wq_words[0].bitcast(I32))
         for quadrant in range(4):
             nc.sync.dma_start(
                 out=w_plane[32 * quadrant : 32 * quadrant + 4, :].bitcast(I32),
                 in_=Wq_scales[0, 4 * quadrant : 4 * quadrant + 4, :].bitcast(I32),
             )
+        nc.sync.dma_start(out=x_run[:, PAIR:GROUP, :], in_=x_steps[:, PAIR:GROUP, :])
         nc.scalar.dma_start(out=k_ext[:, 0:HALO, :], in_=k_before[:, 0:HALO, :])
         nc.scalar.dma_start(out=bias_rows[0:D_BLOCKS, :], in_=bq.rearrange("(c d) -> c d", c=D_BLOCKS))
         nc.scalar.dma_start(out=bias_pairs[0:2, :], in_=bq.rearrange("(u n) -> u n", u=2))
@@ -245,6 +245,19 @@ def tile_crosssliceattention_pa_t_kernel(tc, x, Wq_words, Wq_scales, bq, k_proj,
             scales = quant.tile([P, GROUP * P], U8, align_bytes=64, name="scales")
             nc.vector.quantize_mx(out=codes[:].bitcast(FP8X4), scales=scales[:], in_=grouped_of[g][:])
             quantised_of[g] = (codes, scales)
+
+        def quantise_first_pair(half):
+            if half == 0:
+                codes = quant.tile([P, GROUP * P], U32, align_bytes=64, name="codes")
+                scales = quant.tile([P, GROUP * P], U8, align_bytes=64, name="scales")
+                quantised_of[0] = (codes, scales)
+            codes, scales = quantised_of[0]
+            cols = slice(half * PAIR * P, (half + 1) * PAIR * P)
+            nc.vector.quantize_mx(
+                out=codes[:, cols].bitcast(FP8X4),
+                scales=scales[:, cols],
+                in_=grouped_of[0][:, half * PAIR * P * 4 : (half + 1) * PAIR * P * 4],
+            )
 
         def project(t):
             codes, scales = quantised_of[t // GROUP]
@@ -354,7 +367,7 @@ def tile_crosssliceattention_pa_t_kernel(tc, x, Wq_words, Wq_scales, bq, k_proj,
             codes, scales = band_quantised[s]
             if half == 0:
                 query_cols[s] = work.tile([P, D_BLOCKS, SEQ], F32, name="q_cols")
-            qt = psum_c.tile([P, 2, SEQ], F32, name="qt")
+            qt = psum_t.tile([P, 2, SEQ], F32, name="tp")
             for n in range(2):
                 c = 2 * half + n
                 nc.tensor.matmul_mx(
@@ -508,7 +521,8 @@ def tile_crosssliceattention_pa_t_kernel(tc, x, Wq_words, Wq_scales, bq, k_proj,
             x_at[x_tick(first)] = first
         for g in range(GROUPS):
             last_pair = x_tick(g * GROUP + PAIR)
-            quant_at.setdefault(last_pair if g == 0 else next_gpsimd_tick(last_pair), []).append(g)
+            if g > 0:
+                quant_at.setdefault(next_gpsimd_tick(last_pair), []).append(g)
         for n in range(ROWS // PAIR):
             rows_at[rows_tick(n)] = PAIR * n
         project_tick = 0
@@ -573,6 +587,8 @@ def tile_crosssliceattention_pa_t_kernel(tc, x, Wq_words, Wq_scales, bq, k_proj,
             if 0 <= tick - BAND_END_TICK < len(band_end_phases):
                 band_end_phases[tick - BAND_END_TICK]()
             gate = False
+            if tick < 0:
+                quantise_first_pair(tick - FIRST_TICK)
             for g in quant_at.get(tick, []):
                 quantise_group(g)
                 gate = True

@@ -31,8 +31,6 @@ BAND_TILES = BAND_SEQS * SEQ_TILES
 BAND_TOKENS = BAND_SEQS * SEQ
 WINDOW = P + 2 * HALO
 SLOTS = BAND + 1
-HALF_TILES = BAND_TILES // 2
-HALF_COLS = P // 2
 BAND_NUM = 8
 BAND_DEN = 3
 
@@ -46,6 +44,10 @@ X_LEAD = 2 * GROUP
 GPSIMD_EVERY = 3
 SUM_PLAN = ((3, (0, 1)), (4, (2, 3)), (5, (4,)))
 FIRST_TICK = -2
+EARLY = RUN - GROUP
+END_LAG = 4
+QUADRANT = 32
+QUADRANTS = P // QUADRANT
 LAST_TICK = RUN + 3
 ROWS_SINGLE = 16
 BAND_X_ON_VECTOR = False
@@ -64,6 +66,7 @@ def tile_crosssliceattention_pa_t_kernel(tc, x, Wq_words, Wq_scales, bq, k_proj,
     k_steps = k_flat[BAND_TOKENS:TOKENS, :].rearrange("(p t) d -> p t d", t=RUN)
     k_before = k_flat[BAND_TOKENS - HALO : TOKENS - HALO, :].rearrange("(p t) d -> p t d", t=RUN)
     k_after = k_flat[BAND_TOKENS + RUN : TOKENS, :].rearrange("(p t) d -> p t d", t=RUN)
+    out_band = out_flat[0:BAND_TOKENS, :].rearrange("(t a p) j -> a t (p j)", a=QUADRANTS, p=QUADRANT)
     out_run = out_flat[BAND_TOKENS:TOKENS, :].rearrange("(p t) j -> p (t j)", t=RUN)
 
     with ExitStack() as stack:
@@ -89,6 +92,8 @@ def tile_crosssliceattention_pa_t_kernel(tc, x, Wq_words, Wq_scales, bq, k_proj,
         k_band = keep.tile([P, BAND_TILES, D], BF16)
         raw = keep.tile([P, RUN, SCORE_PAD], F32)
         slots = keep.tile([P, BAND_TILES, SLOTS], F32)
+        flat_weights = keep.tile([P, 2 * P], F32, align_bytes=64)
+        nc.gpsimd.memset(flat_weights[:], 0.0)
         bias_dot = psum_b.tile([P, ROWS], F32)
         key_cols_0 = keep.tile([P, D_BLOCKS, SEQ + 2 * HALO], F32)
         key_cols_1 = keep.tile([P, D_BLOCKS, SEQ + 2 * HALO], F32)
@@ -422,86 +427,6 @@ def tile_crosssliceattention_pa_t_kernel(tc, x, Wq_words, Wq_scales, bq, k_proj,
                 op=ALU.max,
             )
 
-        def exponentials(scores, count, label):
-            top = keep.tile([P, count], F32, name="top_" + label)
-            nc.vector.tensor_reduce(out=top[:], in_=scores[:], axis=AXIS_X, op=ALU.max)
-            weights = keep.tile([P, count, BAND], F32, name="weights_" + label)
-            nc.vector.tensor_tensor(
-                out=weights[:], in0=scores[:], in1=top[:].unsqueeze(2).to_broadcast([P, count, BAND]), op=ALU.subtract
-            )
-            nc.scalar.activation(out=weights[:], in_=weights[:], func=ACT.Exp)
-            return weights
-
-        def inverse_sums(weights, count, label):
-            total = keep.tile([P, count], F32, name="total_" + label)
-            nc.vector.tensor_reduce(out=total[:], in_=weights[:], axis=AXIS_X, op=ALU.add)
-            nc.vector.reciprocal(out=total[:], in_=total[:])
-            return total
-
-        band_end = {}
-
-        def band_end_scores():
-            twice = keep.tile([P, BAND_TILES, 2, SLOTS], F32)
-            nc.vector.tensor_copy(out=twice[:], in_=slots[:].unsqueeze(2).to_broadcast([P, BAND_TILES, 2, SLOTS]))
-            wrapped = twice[:].rearrange("p i w r -> p i (w r)")
-            band_sc = keep.tile([P, BAND_TILES, BAND], F32)
-            nc.vector.tensor_scalar_mul(out=band_sc[:], in0=wrapped[:, :, 0:BAND], scalar1=turn[:, 0:1])
-            for r in range(1, SLOTS):
-                nc.vector.scalar_tensor_tensor(
-                    out=band_sc[:],
-                    in0=wrapped[:, :, r : r + BAND],
-                    scalar=turn[:, r : r + 1],
-                    in1=band_sc[:],
-                    op0=ALU.mult,
-                    op1=ALU.add,
-                )
-            band_end["weights"] = exponentials(band_sc, BAND_TILES, "band")
-
-        def band_end_normalise():
-            weights = band_end["weights"]
-            total = inverse_sums(weights, BAND_TILES, "band")
-            spread = keep.tile([P, 2, 2, HALF_COLS], F32)
-            nc.vector.memset(spread[:], 0.0)
-            for e in range(2):
-                nc.vector.tensor_tensor(
-                    out=spread[:, :, e, 0 : HALF_TILES * BAND].rearrange("p h (t j) -> p h t j", j=BAND),
-                    in0=weights[:].rearrange("p (h t) j -> p h t j", h=2),
-                    in1=total[:].rearrange("p (h t) -> p h t", h=2).unsqueeze(3).to_broadcast([P, 2, HALF_TILES, BAND]),
-                    op=ALU.mult,
-                )
-            t1 = psum_t.tile([P, 2, P], F32, name="tp")
-            for h in range(2):
-                nc.tensor.transpose(t1[:, h, :], spread[:, h, :, :].rearrange("p e m -> p (e m)"), ident[:])
-            band_end["t1"] = t1
-
-        def band_end_pair():
-            t1 = band_end["t1"]
-            paired = keep.tile([P, P], F32)
-            for e in range(2):
-                rows = slice(HALF_COLS * e, HALF_COLS * (e + 1))
-                nc.scalar.copy(out=paired[rows, :].rearrange("m (h u) -> m h u", h=2), in_=t1[rows, :, e:P:2])
-            t2 = psum_t.tile([P, P], F32, name="tp")
-            nc.tensor.transpose(t2[:], paired[:], ident[:])
-            band_end["t2"] = t2
-
-        def band_end_store():
-            t2 = band_end["t2"]
-            band_out = keep.tile([P, HALF_TILES, 2, BAND], F32)
-            nc.scalar.copy(
-                out=band_out[:],
-                in_=t2[:].rearrange("p (e m) -> p e m", e=2)[:, :, 0 : HALF_TILES * BAND].rearrange(
-                    "p e (t j) -> p t e j", j=BAND
-                ),
-            )
-            for h in range(2):
-                tokens = slice(HALF_TILES * P * h, HALF_TILES * P * (h + 1))
-                nc.sync.dma_start(
-                    out=out_flat[tokens, :].rearrange("(t u e) j -> u t (e j)", t=HALF_TILES, e=2),
-                    in_=band_out[HALF_COLS * h : HALF_COLS * (h + 1), :, :, :].rearrange("p t e j -> p t (e j)"),
-                )
-
-        band_end_phases = [band_end_scores, band_end_normalise, band_end_pair, band_end_store]
-
         def is_gpsimd_tick(tick):
             return 0 <= tick < RUN and tick % GPSIMD_EVERY == 1
 
@@ -519,10 +444,12 @@ def tile_crosssliceattention_pa_t_kernel(tc, x, Wq_words, Wq_scales, bq, k_proj,
         band_at = {}
         for first in range(0, RUN, PAIR):
             x_at[x_tick(first)] = first
-        for g in range(GROUPS):
-            last_pair = x_tick(g * GROUP + PAIR)
-            if g > 0:
-                quant_at.setdefault(next_gpsimd_tick(last_pair), []).append(g)
+        def last_gpsimd_tick(tick):
+            while not is_gpsimd_tick(tick):
+                tick -= 1
+            return tick
+        for g in range(1, GROUPS):
+            quant_at.setdefault(last_gpsimd_tick(g * GROUP - 1), []).append(g)
         for n in range(ROWS // PAIR):
             rows_at[rows_tick(n)] = PAIR * n
         project_tick = 0
@@ -534,7 +461,6 @@ def tile_crosssliceattention_pa_t_kernel(tc, x, Wq_words, Wq_scales, bq, k_proj,
             band_at.setdefault(project_tick - 1, []).append(("k", s))
             for depth in range(6):
                 band_at.setdefault(project_tick + depth, []).append((depth, s))
-        BAND_END_TICK = project_tick + 6
 
         for tick in range(FIRST_TICK, LAST_TICK):
             in_run = 0 <= tick < RUN
@@ -584,8 +510,6 @@ def tile_crosssliceattention_pa_t_kernel(tc, x, Wq_words, Wq_scales, bq, k_proj,
             for what, s in band_now:
                 if what == 5:
                     band_extract(s)
-            if 0 <= tick - BAND_END_TICK < len(band_end_phases):
-                band_end_phases[tick - BAND_END_TICK]()
             gate = False
             if tick < 0:
                 quantise_first_pair(tick - FIRST_TICK)
@@ -611,11 +535,91 @@ def tile_crosssliceattention_pa_t_kernel(tc, x, Wq_words, Wq_scales, bq, k_proj,
             if in_run and not on_gpsimd:
                 scores_on_vector(tick, q_ps)
 
-        scores = keep.tile([P, RUN, BAND], F32)
-        nc.vector.tensor_tensor(out=scores[:], in0=raw[:, :, 0:BAND], in1=addend[:], op=ALU.add)
-        weights = exponentials(scores, RUN, "run")
-        total = inverse_sums(weights, RUN, "run")
-        nc.vector.tensor_tensor(
-            out=weights[:], in0=weights[:], in1=total[:].unsqueeze(2).to_broadcast([P, RUN, BAND]), op=ALU.mult
+        def softmax_steps(label, scores, count, dest):
+            top = keep.tile([P, count], F32, name="top_" + label)
+            weights = keep.tile([P, count, BAND], F32, name="weights_" + label)
+            total = keep.tile([P, count], F32, name="total_" + label)
+            return [
+                lambda: nc.vector.tensor_reduce(out=top[:], in_=scores, axis=AXIS_X, op=ALU.max),
+                lambda: nc.vector.tensor_tensor(
+                    out=weights[:], in0=scores, in1=top[:].unsqueeze(2).to_broadcast([P, count, BAND]), op=ALU.subtract
+                ),
+                lambda: nc.scalar.activation(out=weights[:], in_=weights[:], func=ACT.Exp),
+                lambda: nc.vector.tensor_reduce(out=total[:], in_=weights[:], axis=AXIS_X, op=ALU.add),
+                lambda: nc.vector.reciprocal(out=total[:], in_=total[:]),
+                lambda: nc.vector.tensor_tensor(
+                    out=dest, in0=weights[:], in1=total[:].unsqueeze(2).to_broadcast([P, count, BAND]), op=ALU.mult
+                ),
+            ]
+
+        twice = keep.tile([P, BAND_TILES, 2, SLOTS], F32)
+        wrapped = twice[:].rearrange("p i w r -> p i (w r)")
+        band_sc = keep.tile([P, BAND_TILES, BAND], F32)
+        turned = keep.tile([P, 2 * P], F32, align_bytes=64)
+        band_out = keep.tile([P, QUADRANT, BAND], F32)
+
+        def next_turn(r):
+            if r == 0:
+                nc.vector.tensor_scalar_mul(out=band_sc[:], in0=wrapped[:, :, 0:BAND], scalar1=turn[:, 0:1])
+            else:
+                nc.vector.scalar_tensor_tensor(
+                    out=band_sc[:],
+                    in0=wrapped[:, :, r : r + BAND],
+                    scalar=turn[:, r : r + 1],
+                    in1=band_sc[:],
+                    op0=ALU.mult,
+                    op1=ALU.add,
+                )
+
+        def store_band():
+            for a in range(QUADRANTS):
+                nc.sync.dma_start(
+                    out=out_band[a],
+                    in_=band_out[QUADRANT * a : QUADRANT * a + BAND_TILES, :, :].rearrange("t p j -> t (p j)"),
+                )
+
+        band_steps = [
+            lambda: nc.vector.tensor_copy(
+                out=twice[:], in_=slots[:].unsqueeze(2).to_broadcast([P, BAND_TILES, 2, SLOTS])
+            )
+        ]
+        band_steps += [lambda r=r: next_turn(r) for r in range(SLOTS)]
+        band_steps += softmax_steps(
+            "band", band_sc[:], BAND_TILES,
+            flat_weights[:, 0 : BAND * QUADRANT].rearrange("p (j t) -> p t j", j=BAND)[:, 0:BAND_TILES, :],
         )
-        nc.sync.dma_start(out=out_run, in_=weights[:].rearrange("p t j -> p (t j)"))
+        band_steps += [
+            lambda: nc.vector.transpose(out=turned[:], in_=flat_weights[:]),
+            lambda: nc.scalar.copy(
+                out=band_out[:], in_=turned[:, 0 : BAND * QUADRANT].rearrange("q (j p) -> q p j", j=BAND)
+            ),
+            store_band,
+        ]
+
+        scores = keep.tile([P, RUN, BAND], F32)
+        run_weights = keep.tile([P, RUN, BAND], F32)
+
+        def run_steps(first, last):
+            part = slice(first, last)
+            return (
+                [
+                    lambda: nc.vector.tensor_tensor(
+                        out=scores[:, part, :], in0=raw[:, part, 0:BAND], in1=addend[:, part, :], op=ALU.add
+                    )
+                ]
+                + softmax_steps("run%d" % first, scores[:, part, :], last - first, run_weights[:, part, :])
+                + [
+                    lambda: nc.sync.dma_start(
+                        out=out_run[:, first * BAND : last * BAND],
+                        in_=run_weights[:, part, :].rearrange("p t j -> p (t j)"),
+                    )
+                ]
+            )
+
+        run_steps_early = run_steps(0, EARLY)
+        run_steps_late = run_steps(EARLY, RUN)
+        for step in range(len(band_steps)):
+            band_steps[step]()
+            for steps in (run_steps_early, run_steps_late):
+                if 0 <= step - END_LAG < len(steps):
+                    steps[step - END_LAG]()

@@ -44,8 +44,9 @@ X_LEAD = 2 * GROUP
 GPSIMD_EVERY = 3
 SUM_PLAN = ((3, (0, 1)), (4, (2, 3)), (5, (4,)))
 FIRST_TICK = -2
-EARLY = RUN - GROUP
-END_LAG = 4
+BETWEEN = 3
+TURN_TICK = RUN - 2
+END_LAG = 2
 QUADRANT = 32
 QUADRANTS = P // QUADRANT
 LAST_TICK = RUN + 3
@@ -279,8 +280,10 @@ def tile_crosssliceattention_pa_t_kernel(tc, x, Wq_words, Wq_scales, bq, k_proj,
             )
             return q_ps
 
-        def scores_on_vector(t, q_ps):
+        def scores_on_vector(t, q_ps, between=None):
             for j in range(BAND):
+                if between and j == BETWEEN:
+                    between()
                 junk = work.tile([P, D], F32, name="junk")
                 nc.vector.scalar_tensor_tensor(
                     out=junk[:],
@@ -427,6 +430,23 @@ def tile_crosssliceattention_pa_t_kernel(tc, x, Wq_words, Wq_scales, bq, k_proj,
                 op=ALU.max,
             )
 
+        twice = keep.tile([P, BAND_TILES, 2, SLOTS], F32)
+        turned = keep.tile([P, SLOTS, BAND_TILES, BAND], F32)
+        band_sc = keep.tile([P, BAND_TILES, BAND], F32)
+
+        def turn_slots():
+            nc.scalar.copy(out=twice[:], in_=slots[:].unsqueeze(2).to_broadcast([P, BAND_TILES, 2, SLOTS]))
+            wrapped = twice[:].rearrange("p i w r -> p i (w r)")
+            for r in range(SLOTS):
+                nc.scalar.activation(
+                    out=turned[:, r, :, :], in_=wrapped[:, :, r : r + BAND], func=ACT.Copy, scale=turn[:, r : r + 1]
+                )
+
+        def add_turned():
+            nc.vector.tensor_reduce(
+                out=band_sc[:], in_=turned[:].rearrange("p r i j -> p i j r"), axis=AXIS_X, op=ALU.add
+            )
+
         def is_gpsimd_tick(tick):
             return 0 <= tick < RUN and tick % GPSIMD_EVERY == 1
 
@@ -483,15 +503,15 @@ def tile_crosssliceattention_pa_t_kernel(tc, x, Wq_words, Wq_scales, bq, k_proj,
             for lag, neighbours in SUM_PLAN:
                 if tick - lag in products_of:
                     sum_on_scalar(tick - lag, products_of[tick - lag], neighbours)
+            if tick - 2 in rows_of:
+                bias_dot_pair(*rows_of[tick - 2])
+            if tick == 0:
+                prepare_bias()
             for what, s in band_now:
                 if what == 2:
                     band_multiply(s, (0, 1))
                 if what == 3:
                     band_multiply(s, (3, 4))
-            if tick - 2 in rows_of:
-                bias_dot_pair(*rows_of[tick - 2])
-            if tick == 0:
-                prepare_bias()
             if tick in x_at:
                 transpose_run_pair(x_at[tick])
             if tick in rows_at:
@@ -500,13 +520,13 @@ def tile_crosssliceattention_pa_t_kernel(tc, x, Wq_words, Wq_scales, bq, k_proj,
                 if what == "x":
                     band_x(s)
             for what, s in band_now:
+                if what == "k":
+                    band_k(s)
+            for what, s in band_now:
                 if what == 2:
                     band_multiply(s, (2,))
                 if what == 3:
                     band_multiply(s, (5,))
-            for what, s in band_now:
-                if what == "k":
-                    band_k(s)
             for what, s in band_now:
                 if what == 5:
                     band_extract(s)
@@ -533,7 +553,9 @@ def tile_crosssliceattention_pa_t_kernel(tc, x, Wq_words, Wq_scales, bq, k_proj,
                         op1=ALU.add,
                     )
             if in_run and not on_gpsimd:
-                scores_on_vector(tick, q_ps)
+                scores_on_vector(tick, q_ps, add_turned if tick == RUN - 1 else None)
+            if tick == TURN_TICK:
+                turn_slots()
 
         def softmax_steps(label, scores, count, dest):
             top = keep.tile([P, count], F32, name="top_" + label)
@@ -552,74 +574,38 @@ def tile_crosssliceattention_pa_t_kernel(tc, x, Wq_words, Wq_scales, bq, k_proj,
                 ),
             ]
 
-        twice = keep.tile([P, BAND_TILES, 2, SLOTS], F32)
-        wrapped = twice[:].rearrange("p i w r -> p i (w r)")
-        band_sc = keep.tile([P, BAND_TILES, BAND], F32)
-        turned = keep.tile([P, 2 * P], F32, align_bytes=64)
+        flat_turned = keep.tile([P, 2 * P], F32, align_bytes=64)
         band_out = keep.tile([P, QUADRANT, BAND], F32)
-
-        def next_turn(r):
-            if r == 0:
-                nc.vector.tensor_scalar_mul(out=band_sc[:], in0=wrapped[:, :, 0:BAND], scalar1=turn[:, 0:1])
-            else:
-                nc.vector.scalar_tensor_tensor(
-                    out=band_sc[:],
-                    in0=wrapped[:, :, r : r + BAND],
-                    scalar=turn[:, r : r + 1],
-                    in1=band_sc[:],
-                    op0=ALU.mult,
-                    op1=ALU.add,
-                )
 
         def store_band():
             for a in range(QUADRANTS):
-                nc.sync.dma_start(
+                queue = nc.sync if a % 2 == 0 else nc.scalar
+                queue.dma_start(
                     out=out_band[a],
                     in_=band_out[QUADRANT * a : QUADRANT * a + BAND_TILES, :, :].rearrange("t p j -> t (p j)"),
                 )
 
-        band_steps = [
-            lambda: nc.vector.tensor_copy(
-                out=twice[:], in_=slots[:].unsqueeze(2).to_broadcast([P, BAND_TILES, 2, SLOTS])
-            )
-        ]
-        band_steps += [lambda r=r: next_turn(r) for r in range(SLOTS)]
-        band_steps += softmax_steps(
+        band_steps = softmax_steps(
             "band", band_sc[:], BAND_TILES,
             flat_weights[:, 0 : BAND * QUADRANT].rearrange("p (j t) -> p t j", j=BAND)[:, 0:BAND_TILES, :],
         )
         band_steps += [
-            lambda: nc.vector.transpose(out=turned[:], in_=flat_weights[:]),
+            lambda: nc.vector.transpose(out=flat_turned[:], in_=flat_weights[:]),
             lambda: nc.scalar.copy(
-                out=band_out[:], in_=turned[:, 0 : BAND * QUADRANT].rearrange("q (j p) -> q p j", j=BAND)
+                out=band_out[:], in_=flat_turned[:, 0 : BAND * QUADRANT].rearrange("q (j p) -> q p j", j=BAND)
             ),
             store_band,
         ]
 
         scores = keep.tile([P, RUN, BAND], F32)
         run_weights = keep.tile([P, RUN, BAND], F32)
-
-        def run_steps(first, last):
-            part = slice(first, last)
-            return (
-                [
-                    lambda: nc.vector.tensor_tensor(
-                        out=scores[:, part, :], in0=raw[:, part, 0:BAND], in1=addend[:, part, :], op=ALU.add
-                    )
-                ]
-                + softmax_steps("run%d" % first, scores[:, part, :], last - first, run_weights[:, part, :])
-                + [
-                    lambda: nc.sync.dma_start(
-                        out=out_run[:, first * BAND : last * BAND],
-                        in_=run_weights[:, part, :].rearrange("p t j -> p (t j)"),
-                    )
-                ]
-            )
-
-        run_steps_early = run_steps(0, EARLY)
-        run_steps_late = run_steps(EARLY, RUN)
-        for step in range(len(band_steps)):
-            band_steps[step]()
-            for steps in (run_steps_early, run_steps_late):
-                if 0 <= step - END_LAG < len(steps):
-                    steps[step - END_LAG]()
+        run_steps = [
+            lambda: nc.vector.tensor_tensor(out=scores[:], in0=raw[:, :, 0:BAND], in1=addend[:], op=ALU.add)
+        ]
+        run_steps += softmax_steps("run", scores[:], RUN, run_weights[:])
+        run_steps += [lambda: nc.sync.dma_start(out=out_run, in_=run_weights[:].rearrange("p t j -> p (t j)"))]
+        for step in range(max(len(band_steps), END_LAG + len(run_steps))):
+            if step < len(band_steps):
+                band_steps[step]()
+            if 0 <= step - END_LAG < len(run_steps):
+                run_steps[step - END_LAG]()

@@ -44,9 +44,7 @@ X_LEAD = 2 * GROUP
 GPSIMD_EVERY = 3
 SUM_PLAN = ((3, (0, 1)), (4, (2, 3)), (5, (4,)))
 FIRST_TICK = -2
-BETWEEN = 3
 TURN_TICK = RUN - 2
-END_LAG = 2
 QUADRANT = 32
 QUADRANTS = P // QUADRANT
 LAST_TICK = RUN + 3
@@ -102,7 +100,7 @@ def tile_crosssliceattention_pa_t_kernel(tc, x, Wq_words, Wq_scales, bq, k_proj,
         key_cols = [key_cols_0, key_cols_1, key_cols_2]
 
         nc.vector.memset(w_plane[:].bitcast(I32), 0)
-        nc.vector.memset(k_ext[:, RUN + HALO :, :], 0.0)
+        nc.gpsimd.memset(k_ext[:, RUN + HALO :, :], 0.0)
         nc.vector.memset(bias_rows[:], 0.0)
         nc.vector.memset(bias_pairs[:], 0.0)
         warm = keep.tile([P, 1], F32)
@@ -191,8 +189,6 @@ def tile_crosssliceattention_pa_t_kernel(tc, x, Wq_words, Wq_scales, bq, k_proj,
         nc.scalar.dma_start(out=k_ext[:, 0:HALO, :], in_=k_before[:, 0:HALO, :])
         nc.scalar.dma_start(out=bias_rows[0:D_BLOCKS, :], in_=bq.rearrange("(c d) -> c d", c=D_BLOCKS))
         nc.scalar.dma_start(out=bias_pairs[0:2, :], in_=bq.rearrange("(u n) -> u n", u=2))
-        nc.scalar.dma_start(out=k_ext[0:112, RUN + HALO :, :], in_=k_after[0:112, 0:HALO, :])
-        nc.scalar.dma_start(out=k_ext[112 : P - 1, RUN + HALO :, :], in_=k_after[112 : P - 1, 0:HALO, :])
         loads = []
         for g in range(1, GROUPS):
             loads.append((x_tick(g * GROUP), 0, load_x_run, g))
@@ -203,6 +199,8 @@ def tile_crosssliceattention_pa_t_kernel(tc, x, Wq_words, Wq_scales, bq, k_proj,
             loads.append((band_tick(2 * n) + 1, 3, load_k_band, n))
         for entry in sorted(loads, key=lambda item: (item[0], item[1])):
             entry[2](entry[3])
+        nc.sync.dma_start(out=k_ext[0:112, RUN + HALO :, :], in_=k_after[0:112, 0:HALO, :])
+        nc.sync.dma_start(out=k_ext[112 : P - 1, RUN + HALO :, :], in_=k_after[112 : P - 1, 0:HALO, :])
 
         bias = {}
 
@@ -280,10 +278,10 @@ def tile_crosssliceattention_pa_t_kernel(tc, x, Wq_words, Wq_scales, bq, k_proj,
             )
             return q_ps
 
-        def scores_on_vector(t, q_ps, between=None):
+        def scores_on_vector(t, q_ps, between):
             for j in range(BAND):
-                if between and j == BETWEEN:
-                    between()
+                for function in between.get(j, []):
+                    function()
                 junk = work.tile([P, D], F32, name="junk")
                 nc.vector.scalar_tensor_tensor(
                     out=junk[:],
@@ -420,9 +418,11 @@ def tile_crosssliceattention_pa_t_kernel(tc, x, Wq_words, Wq_scales, bq, k_proj,
                     stop=(c == D_BLOCKS - 1),
                 )
 
-        def band_extract(s):
+        def band_mask_scores(s):
             masked_of[s] = work.tile([P, SEQ_TILES, WINDOW], F32, name="masked")
             nc.vector.tensor_tensor(out=masked_of[s][:], in0=sc_of[s % 2][:], in1=band_mask[:], op=ALU.add)
+
+        def band_pick(s):
             nc.vector.tensor_reduce(
                 out=slots[:, SEQ_TILES * s : SEQ_TILES * (s + 1), :],
                 in_=masked_of[s][:].rearrange("p i (a r) -> p i r a", r=SLOTS),
@@ -430,22 +430,66 @@ def tile_crosssliceattention_pa_t_kernel(tc, x, Wq_words, Wq_scales, bq, k_proj,
                 op=ALU.max,
             )
 
+        def softmax_steps(label, scores, weights, dest, count, by_token, over_neighbours):
+            top = keep.tile([P, count], F32, name="top_" + label)
+            total = keep.tile([P, count], F32, name="total_" + label)
+            return [
+                lambda: nc.vector.tensor_reduce(out=top[:], in_=by_token(scores), axis=AXIS_X, op=ALU.max),
+                lambda: nc.vector.tensor_tensor(out=weights, in0=scores, in1=over_neighbours(top[:]), op=ALU.subtract),
+                lambda: nc.scalar.activation(out=weights, in_=weights, func=ACT.Exp),
+                lambda: nc.vector.tensor_reduce(out=total[:], in_=by_token(weights), axis=AXIS_X, op=ALU.add),
+                lambda: nc.vector.reciprocal(out=total[:], in_=total[:]),
+                lambda: nc.vector.tensor_tensor(out=dest, in0=weights, in1=over_neighbours(total[:]), op=ALU.mult),
+            ]
+
         twice = keep.tile([P, BAND_TILES, 2, SLOTS], F32)
-        turned = keep.tile([P, SLOTS, BAND_TILES, BAND], F32)
-        band_sc = keep.tile([P, BAND_TILES, BAND], F32)
+        turned = keep.tile([P, SLOTS, BAND, BAND_TILES], F32)
+        band_sc = keep.tile([P, BAND, BAND_TILES], F32)
 
         def turn_slots():
             nc.scalar.copy(out=twice[:], in_=slots[:].unsqueeze(2).to_broadcast([P, BAND_TILES, 2, SLOTS]))
             wrapped = twice[:].rearrange("p i w r -> p i (w r)")
             for r in range(SLOTS):
                 nc.scalar.activation(
-                    out=turned[:, r, :, :], in_=wrapped[:, :, r : r + BAND], func=ACT.Copy, scale=turn[:, r : r + 1]
+                    out=turned[:, r, :, :],
+                    in_=wrapped[:, :, r : r + BAND].rearrange("p i j -> p j i"),
+                    func=ACT.Copy,
+                    scale=turn[:, r : r + 1],
                 )
 
         def add_turned():
             nc.vector.tensor_reduce(
-                out=band_sc[:], in_=turned[:].rearrange("p r i j -> p i j r"), axis=AXIS_X, op=ALU.add
+                out=band_sc[:], in_=turned[:].rearrange("p r j i -> p j i r"), axis=AXIS_X, op=ALU.add
             )
+
+        band_weights = keep.tile([P, BAND, BAND_TILES], F32)
+        flat_turned = keep.tile([P, 2 * P], F32, align_bytes=64)
+        band_out = keep.tile([P, QUADRANT, BAND], F32)
+
+        def store_band():
+            for a in range(QUADRANTS):
+                queue = nc.sync if a % 2 == 0 else nc.scalar
+                queue.dma_start(
+                    out=out_band[a],
+                    in_=band_out[QUADRANT * a : QUADRANT * a + BAND_TILES, :, :].rearrange("t p j -> t (p j)"),
+                )
+
+        band_steps = softmax_steps(
+            "band",
+            band_sc[:],
+            band_weights[:],
+            flat_weights[:, 0 : BAND * QUADRANT].rearrange("p (j t) -> p j t", j=BAND)[:, :, 0:BAND_TILES],
+            BAND_TILES,
+            lambda view: view.rearrange("p j i -> p i j"),
+            lambda stat: stat.unsqueeze(1).to_broadcast([P, BAND, BAND_TILES]),
+        )
+        band_steps += [
+            lambda: nc.vector.transpose(out=flat_turned[:], in_=flat_weights[:]),
+            lambda: nc.scalar.copy(
+                out=band_out[:], in_=flat_turned[:, 0 : BAND * QUADRANT].rearrange("q (j p) -> q p j", j=BAND)
+            ),
+            store_band,
+        ]
 
         def is_gpsimd_tick(tick):
             return 0 <= tick < RUN and tick % GPSIMD_EVERY == 1
@@ -456,6 +500,10 @@ def tile_crosssliceattention_pa_t_kernel(tc, x, Wq_words, Wq_scales, bq, k_proj,
             return tick
 
         products_of = {}
+        q_of = {}
+        project_at = {}
+        for t in range(RUN):
+            project_at.setdefault(t - 1 if 0 < t <= 1 else t, []).append(t)
         rows_of = {}
         addend = keep.tile([P, RUN, BAND], F32)
         x_at = {}
@@ -488,8 +536,10 @@ def tile_crosssliceattention_pa_t_kernel(tc, x, Wq_words, Wq_scales, bq, k_proj,
             band_now = band_at.get(tick, [])
             q_ps = None
             q_sb = None
+            for t in project_at.get(tick, []):
+                q_of[t] = project(t)
             if in_run:
-                q_ps = project(tick)
+                q_ps = q_of[tick]
             if on_gpsimd:
                 q_sb = copy_for_gpsimd(q_ps)
             for what, s in band_now:
@@ -527,9 +577,12 @@ def tile_crosssliceattention_pa_t_kernel(tc, x, Wq_words, Wq_scales, bq, k_proj,
                     band_multiply(s, (2,))
                 if what == 3:
                     band_multiply(s, (5,))
+            picks = []
+            between = {}
             for what, s in band_now:
                 if what == 5:
-                    band_extract(s)
+                    band_mask_scores(s)
+                    picks.append(lambda s=s: band_pick(s))
             gate = False
             if tick < 0:
                 quantise_first_pair(tick - FIRST_TICK)
@@ -552,60 +605,30 @@ def tile_crosssliceattention_pa_t_kernel(tc, x, Wq_words, Wq_scales, bq, k_proj,
                         op0=ALU.mult,
                         op1=ALU.add,
                     )
+            if tick == RUN - 1:
+                picks.append(add_turned)
+                between = {2: [band_steps[0]], 4: [band_steps[1]]}
             if in_run and not on_gpsimd:
-                scores_on_vector(tick, q_ps, add_turned if tick == RUN - 1 else None)
+                scores_on_vector(tick, q_ps, dict([(1, picks)] + list(between.items())))
+            else:
+                for pick in picks:
+                    pick()
             if tick == TURN_TICK:
                 turn_slots()
-
-        def softmax_steps(label, scores, count, dest):
-            top = keep.tile([P, count], F32, name="top_" + label)
-            weights = keep.tile([P, count, BAND], F32, name="weights_" + label)
-            total = keep.tile([P, count], F32, name="total_" + label)
-            return [
-                lambda: nc.vector.tensor_reduce(out=top[:], in_=scores, axis=AXIS_X, op=ALU.max),
-                lambda: nc.vector.tensor_tensor(
-                    out=weights[:], in0=scores, in1=top[:].unsqueeze(2).to_broadcast([P, count, BAND]), op=ALU.subtract
-                ),
-                lambda: nc.scalar.activation(out=weights[:], in_=weights[:], func=ACT.Exp),
-                lambda: nc.vector.tensor_reduce(out=total[:], in_=weights[:], axis=AXIS_X, op=ALU.add),
-                lambda: nc.vector.reciprocal(out=total[:], in_=total[:]),
-                lambda: nc.vector.tensor_tensor(
-                    out=dest, in0=weights[:], in1=total[:].unsqueeze(2).to_broadcast([P, count, BAND]), op=ALU.mult
-                ),
-            ]
-
-        flat_turned = keep.tile([P, 2 * P], F32, align_bytes=64)
-        band_out = keep.tile([P, QUADRANT, BAND], F32)
-
-        def store_band():
-            for a in range(QUADRANTS):
-                queue = nc.sync if a % 2 == 0 else nc.scalar
-                queue.dma_start(
-                    out=out_band[a],
-                    in_=band_out[QUADRANT * a : QUADRANT * a + BAND_TILES, :, :].rearrange("t p j -> t (p j)"),
-                )
-
-        band_steps = softmax_steps(
-            "band", band_sc[:], BAND_TILES,
-            flat_weights[:, 0 : BAND * QUADRANT].rearrange("p (j t) -> p t j", j=BAND)[:, 0:BAND_TILES, :],
-        )
-        band_steps += [
-            lambda: nc.vector.transpose(out=flat_turned[:], in_=flat_weights[:]),
-            lambda: nc.scalar.copy(
-                out=band_out[:], in_=flat_turned[:, 0 : BAND * QUADRANT].rearrange("q (j p) -> q p j", j=BAND)
-            ),
-            store_band,
-        ]
 
         scores = keep.tile([P, RUN, BAND], F32)
         run_weights = keep.tile([P, RUN, BAND], F32)
         run_steps = [
             lambda: nc.vector.tensor_tensor(out=scores[:], in0=raw[:, :, 0:BAND], in1=addend[:], op=ALU.add)
         ]
-        run_steps += softmax_steps("run", scores[:], RUN, run_weights[:])
+        run_steps += softmax_steps(
+            "run", scores[:], run_weights[:], run_weights[:], RUN,
+            lambda view: view,
+            lambda stat: stat.unsqueeze(2).to_broadcast([P, RUN, BAND]),
+        )
         run_steps += [lambda: nc.sync.dma_start(out=out_run, in_=run_weights[:].rearrange("p t j -> p (t j)"))]
-        for step in range(max(len(band_steps), END_LAG + len(run_steps))):
-            if step < len(band_steps):
-                band_steps[step]()
-            if 0 <= step - END_LAG < len(run_steps):
-                run_steps[step - END_LAG]()
+        band_steps[2]()
+        for step, run_step in enumerate(run_steps):
+            run_step()
+            if step + 3 < len(band_steps):
+                band_steps[step + 3]()

@@ -92,7 +92,6 @@ def tile_crosssliceattention_pa_t_kernel(tc, x, Wq_words, Wq_scales, bq, k_proj,
         raw = keep.tile([P, RUN, SCORE_PAD], F32)
         slots = keep.tile([P, BAND_TILES, SLOTS], F32)
         flat_weights = keep.tile([P, 2 * P], F32, align_bytes=64)
-        nc.gpsimd.memset(flat_weights[:], 0.0)
         bias_dot = psum_b.tile([P, ROWS], F32)
         key_cols_0 = keep.tile([P, D_BLOCKS, SEQ + 2 * HALO], F32)
         key_cols_1 = keep.tile([P, D_BLOCKS, SEQ + 2 * HALO], F32)
@@ -100,7 +99,6 @@ def tile_crosssliceattention_pa_t_kernel(tc, x, Wq_words, Wq_scales, bq, k_proj,
         key_cols = [key_cols_0, key_cols_1, key_cols_2]
 
         nc.vector.memset(w_plane[:].bitcast(I32), 0)
-        nc.gpsimd.memset(k_ext[:, RUN + HALO :, :], 0.0)
         nc.vector.memset(bias_rows[:], 0.0)
         nc.vector.memset(bias_pairs[:], 0.0)
         warm = keep.tile([P, 1], F32)
@@ -151,8 +149,11 @@ def tile_crosssliceattention_pa_t_kernel(tc, x, Wq_words, Wq_scales, bq, k_proj,
                 op0=ALU.is_gt, op1=ALU.mult,
             )
 
+        nc.gpsimd.memset(k_ext[:, RUN + HALO :, :], 0.0)
+        nc.gpsimd.memset(flat_weights[:], 0.0)
+
         def x_tick(first):
-            return max(first - X_LEAD, first // 2 + FIRST_TICK)
+            return max(first - X_LEAD, first // 2 + FIRST_TICK - (1 if first == GROUP + PAIR else 0))
 
         def band_tick(s):
             return (s * BAND_NUM) // BAND_DEN
@@ -180,15 +181,13 @@ def tile_crosssliceattention_pa_t_kernel(tc, x, Wq_words, Wq_scales, bq, k_proj,
 
         nc.sync.dma_start(out=x_run[:, 0:PAIR, :], in_=x_steps[:, 0:PAIR, :])
         nc.sync.dma_start(out=w_words[:].bitcast(I32), in_=Wq_words[0].bitcast(I32))
+        nc.sync.dma_start(out=x_run[:, PAIR:GROUP, :], in_=x_steps[:, PAIR:GROUP, :])
         for quadrant in range(4):
             nc.sync.dma_start(
                 out=w_plane[32 * quadrant : 32 * quadrant + 4, :].bitcast(I32),
                 in_=Wq_scales[0, 4 * quadrant : 4 * quadrant + 4, :].bitcast(I32),
             )
-        nc.sync.dma_start(out=x_run[:, PAIR:GROUP, :], in_=x_steps[:, PAIR:GROUP, :])
         nc.scalar.dma_start(out=k_ext[:, 0:HALO, :], in_=k_before[:, 0:HALO, :])
-        nc.scalar.dma_start(out=bias_rows[0:D_BLOCKS, :], in_=bq.rearrange("(c d) -> c d", c=D_BLOCKS))
-        nc.scalar.dma_start(out=bias_pairs[0:2, :], in_=bq.rearrange("(u n) -> u n", u=2))
         loads = []
         for g in range(1, GROUPS):
             loads.append((x_tick(g * GROUP), 0, load_x_run, g))
@@ -197,6 +196,11 @@ def tile_crosssliceattention_pa_t_kernel(tc, x, Wq_words, Wq_scales, bq, k_proj,
         for n in range(BAND_SEQS // 2):
             loads.append((band_tick(2 * n), 2, load_x_band, n))
             loads.append((band_tick(2 * n) + 1, 3, load_k_band, n))
+        def load_bias(n):
+            nc.sync.dma_start(out=bias_rows[0:D_BLOCKS, :], in_=bq.rearrange("(c d) -> c d", c=D_BLOCKS))
+            nc.sync.dma_start(out=bias_pairs[0:2, :], in_=bq.rearrange("(u n) -> u n", u=2))
+
+        loads.append((x_tick(GROUP), 1, load_bias, 0))
         for entry in sorted(loads, key=lambda item: (item[0], item[1])):
             entry[2](entry[3])
         nc.sync.dma_start(out=k_ext[0:112, RUN + HALO :, :], in_=k_after[0:112, 0:HALO, :])
@@ -404,16 +408,20 @@ def tile_crosssliceattention_pa_t_kernel(tc, x, Wq_words, Wq_scales, bq, k_proj,
         sc_0 = psum_s.tile([P, SEQ_TILES, WINDOW], F32)
         sc_1 = psum_s.tile([P, SEQ_TILES, WINDOW], F32)
         sc_of = [sc_0, sc_1]
+        for scores in sc_of:
+            nc.tensor.transpose(scores[:, 0, 0:P], ident[:], ident[:])
+            nc.tensor.transpose(scores[:, 1, WINDOW - P : WINDOW], ident[:], ident[:])
         masked_of = {}
 
         def band_multiply(s, parts):
             cols = key_cols[s % len(key_cols)]
             for part in parts:
                 i, c = divmod(part, D_BLOCKS)
+                inside = slice(HALO if i == 0 else 0, WINDOW - HALO if i == SEQ_TILES - 1 else WINDOW)
                 nc.tensor.matmul(
-                    out=sc_of[s % 2][:, i, :],
+                    out=sc_of[s % 2][:, i, inside],
                     lhsT=query_cols[s][:, c, i * P : (i + 1) * P],
-                    rhs=cols[:, c, i * P : i * P + WINDOW],
+                    rhs=cols[:, c, i * P + inside.start : i * P + inside.stop],
                     start=(c == 0),
                     stop=(c == D_BLOCKS - 1),
                 )
@@ -511,7 +519,7 @@ def tile_crosssliceattention_pa_t_kernel(tc, x, Wq_words, Wq_scales, bq, k_proj,
         rows_at = {}
         band_at = {}
         for first in range(0, RUN, PAIR):
-            x_at[x_tick(first)] = first
+            x_at.setdefault(x_tick(first), []).append(first)
         def last_gpsimd_tick(tick):
             while not is_gpsimd_tick(tick):
                 tick -= 1
@@ -562,8 +570,8 @@ def tile_crosssliceattention_pa_t_kernel(tc, x, Wq_words, Wq_scales, bq, k_proj,
                     band_multiply(s, (0, 1))
                 if what == 3:
                     band_multiply(s, (3, 4))
-            if tick in x_at:
-                transpose_run_pair(x_at[tick])
+            for first in x_at.get(tick, []):
+                transpose_run_pair(first)
             if tick in rows_at:
                 rows_of[tick] = (rows_at[tick], transpose_rows(rows_at[tick]))
             for what, s in band_now:

@@ -43,6 +43,8 @@ SCORE_PAD = 8
 X_LEAD = 2 * GROUP
 GPSIMD_EVERY = 3
 SUM_PLAN = ((3, (0, 1)), (4, (2, 3)), (5, (4,)))
+X_GROUPS_HELD = 7
+JUNK_BUFFERS = 16
 FIRST_TICK = -2
 TURN_TICK = RUN - 2
 QUADRANT = 32
@@ -73,6 +75,7 @@ def tile_crosssliceattention_pa_t_kernel(tc, x, Wq_words, Wq_scales, bq, k_proj,
         keep = stack.enter_context(tc.tile_pool(name="keep", bufs=1))
         quant = stack.enter_context(tc.tile_pool(name="quant", bufs=3))
         rows_pool = stack.enter_context(tc.tile_pool(name="rows_pool", bufs=3))
+        x_pool = stack.enter_context(tc.tile_pool(name="x_pool", bufs=X_GROUPS_HELD))
         work = stack.enter_context(tc.tile_pool(name="work", bufs=2))
         psum_t = stack.enter_context(tc.psum_pool(name="psum_t", bufs=3))
         psum_q = stack.enter_context(tc.psum_pool(name="psum_q", bufs=2))
@@ -85,7 +88,6 @@ def tile_crosssliceattention_pa_t_kernel(tc, x, Wq_words, Wq_scales, bq, k_proj,
         ident_bf = keep.tile([P, P], BF16)
         bias_rows = keep.tile([P, P], BF16)
         bias_pairs = keep.tile([P, 2 * P], BF16)
-        x_run = keep.tile([P, RUN, D], BF16)
         k_ext = keep.tile([P, ROWS, D], BF16)
         x_band = keep.tile([P, BAND_TILES, D], BF16)
         k_band = keep.tile([P, BAND_TILES, D], BF16)
@@ -163,7 +165,8 @@ def tile_crosssliceattention_pa_t_kernel(tc, x, Wq_words, Wq_scales, bq, k_proj,
 
         def load_x_run(g):
             steps = slice(g * GROUP, (g + 1) * GROUP)
-            nc.sync.dma_start(out=x_run[:, steps, :], in_=x_steps[:, steps, :])
+            x_groups[g] = x_pool.tile([P, GROUP, D], BF16, name="x_run")
+            nc.sync.dma_start(out=x_groups[g][:], in_=x_steps[:, steps, :])
 
         def load_k_run(g):
             nc.sync.dma_start(
@@ -179,9 +182,11 @@ def tile_crosssliceattention_pa_t_kernel(tc, x, Wq_words, Wq_scales, bq, k_proj,
             tiles = slice(2 * SEQ_TILES * n, 2 * SEQ_TILES * (n + 1))
             nc.sync.dma_start(out=k_band[:, tiles, :], in_=k_tiles[:, tiles, :])
 
-        nc.sync.dma_start(out=x_run[:, 0:PAIR, :], in_=x_steps[:, 0:PAIR, :])
+        x_first = x_pool.tile([P, GROUP, D], BF16, name="x_run")
+        x_groups = {0: x_first}
+        nc.sync.dma_start(out=x_first[:, 0:PAIR, :], in_=x_steps[:, 0:PAIR, :])
         nc.sync.dma_start(out=w_words[:].bitcast(I32), in_=Wq_words[0].bitcast(I32))
-        nc.sync.dma_start(out=x_run[:, PAIR:GROUP, :], in_=x_steps[:, PAIR:GROUP, :])
+        nc.sync.dma_start(out=x_first[:, PAIR:GROUP, :], in_=x_steps[:, PAIR:GROUP, :])
         for quadrant in range(4):
             nc.sync.dma_start(
                 out=w_plane[32 * quadrant : 32 * quadrant + 4, :].bitcast(I32),
@@ -189,7 +194,7 @@ def tile_crosssliceattention_pa_t_kernel(tc, x, Wq_words, Wq_scales, bq, k_proj,
             )
         nc.scalar.dma_start(out=k_ext[:, 0:HALO, :], in_=k_before[:, 0:HALO, :])
         loads = []
-        for g in range(1, GROUPS):
+        for g in range(1, X_GROUPS_HELD):
             loads.append((x_tick(g * GROUP), 0, load_x_run, g))
         for g in range(GROUPS):
             loads.append((g * GROUP - HALO - 1, 1, load_k_run, g))
@@ -224,7 +229,6 @@ def tile_crosssliceattention_pa_t_kernel(tc, x, Wq_words, Wq_scales, bq, k_proj,
             flat = tile_ap.rearrange("p t k -> p (t k)").bitcast(F32)
             return flat.rearrange("p (t w) -> p t w", t=count)
 
-        x_run_words = words_of(x_run[:], RUN)
         x_band_words = words_of(x_band[:], BAND_TILES)
         k_words = words_of(k_ext[:], ROWS)
 
@@ -246,7 +250,7 @@ def tile_crosssliceattention_pa_t_kernel(tc, x, Wq_words, Wq_scales, bq, k_proj,
             if first % GROUP == 0:
                 grouped_of[g] = quant.tile([P, GROUP * P * 4], BF16, align_bytes=64, name="grouped")
             grouped_words = grouped_of[g][:].bitcast(F32).rearrange("q (t p u) -> q t p u", t=GROUP, u=2)
-            transpose_x_pair(x_run_words, first, grouped_words[:, first % GROUP : first % GROUP + PAIR, :, :])
+            transpose_x_pair(words_of(x_groups[g][:], GROUP), first % GROUP, grouped_words[:, first % GROUP : first % GROUP + PAIR, :, :])
 
         def quantise_group(g):
             codes = quant.tile([P, GROUP * P], U32, align_bytes=64, name="codes")
@@ -286,7 +290,7 @@ def tile_crosssliceattention_pa_t_kernel(tc, x, Wq_words, Wq_scales, bq, k_proj,
             for j in range(BAND):
                 for function in between.get(j, []):
                     function()
-                junk = work.tile([P, D], F32, name="junk")
+                junk = work.tile([P, D], BF16, name="junk", bufs=JUNK_BUFFERS)
                 nc.vector.scalar_tensor_tensor(
                     out=junk[:],
                     in0=q_ps[:],
@@ -572,6 +576,9 @@ def tile_crosssliceattention_pa_t_kernel(tc, x, Wq_words, Wq_scales, bq, k_proj,
                     band_multiply(s, (3, 4))
             for first in x_at.get(tick, []):
                 transpose_run_pair(first)
+                g = first // GROUP + X_GROUPS_HELD
+                if first % GROUP == GROUP - PAIR and g < GROUPS:
+                    load_x_run(g)
             if tick in rows_at:
                 rows_of[tick] = (rows_at[tick], transpose_rows(rows_at[tick]))
             for what, s in band_now:

import math
from contextlib import ExitStack

import concourse.mybir as mybir
from concourse.masks import make_identity

F32 = mybir.dt.float32
BF16 = mybir.dt.bfloat16
I32 = mybir.dt.int32
U32 = mybir.dt.uint32
U8 = mybir.dt.uint8
FP8X4 = mybir.dt.float8_e4m3fn_x4
FP4X4 = mybir.dt.float4_e2m1fn_x4
ALU = mybir.AluOpType
ACT = mybir.ActivationFunctionType
AXIS_X = mybir.AxisListType.X

P = 128
TOKENS = 32 * 256
SEQ = 256
D = 512
D_BLOCKS = D // P
HALO = 2
BAND = 2 * HALO + 1
INV_SQRT_D = 1.0 / math.sqrt(D)
MASKED = -1.0e30

BAND_SEQS = 12
SEQ_TILES = SEQ // P
BAND_TILES = BAND_SEQS * SEQ_TILES
BAND_TOKENS = BAND_SEQS * SEQ
WINDOW = P + 2 * HALO
SLOTS = BAND + 1
BAND_NUM = 8
BAND_DEN = 3

RUN = (TOKENS - BAND_TOKENS) // P
ROWS = RUN + 2 * HALO
GROUP = 4
GROUPS = RUN // GROUP
PAIR = 2
SCORE_PAD = 8
X_LEAD = 2 * GROUP
GPSIMD_EVERY = 3
SUM_PLAN = ((3, (0, 1)), (4, (2, 3)), (5, (4,)))
X_GROUPS_HELD = 7
JUNK_BUFFERS = 16
FIRST_TICK = -2
TURN_TICK = RUN - 2
QUADRANT = 32
QUADRANTS = P // QUADRANT
LAST_TICK = RUN + 3
ROWS_SINGLE = 16
BAND_X_ON_VECTOR = False

FLOPS = 2 * TOKENS * D * D + 2 * TOKENS * BAND * D


def tile_crosssliceattention_pa_t_kernel(tc, x, Wq_words, Wq_scales, bq, k_proj, out):
    nc = tc.nc
    x_flat = x.flatten_outer_dims()
    k_flat = k_proj.flatten_outer_dims()
    out_flat = out.flatten_outer_dims()
    x_tiles = x_flat[0:BAND_TOKENS, :].rearrange("(i p) k -> p i k", p=P)
    k_tiles = k_flat[0:BAND_TOKENS, :].rearrange("(i p) d -> p i d", p=P)
    x_steps = x_flat[BAND_TOKENS:TOKENS, :].rearrange("(p t) k -> p t k", t=RUN)
    k_steps = k_flat[BAND_TOKENS:TOKENS, :].rearrange("(p t) d -> p t d", t=RUN)
    k_before = k_flat[BAND_TOKENS - HALO : TOKENS - HALO, :].rearrange("(p t) d -> p t d", t=RUN)
    k_after = k_flat[BAND_TOKENS + RUN : TOKENS, :].rearrange("(p t) d -> p t d", t=RUN)
    out_band = out_flat[0:BAND_TOKENS, :].rearrange("(t a p) j -> a t (p j)", a=QUADRANTS, p=QUADRANT)
    out_run = out_flat[BAND_TOKENS:TOKENS, :].rearrange("(p t) j -> p (t j)", t=RUN)

    with ExitStack() as stack:
        stack.enter_context(tc.manual_schedule())
        keep = stack.enter_context(tc.tile_pool(name="keep", bufs=1))
        quant = stack.enter_context(tc.tile_pool(name="quant", bufs=3))
        rows_pool = stack.enter_context(tc.tile_pool(name="rows_pool", bufs=3))
        x_pool = stack.enter_context(tc.tile_pool(name="x_pool", bufs=X_GROUPS_HELD))
        work = stack.enter_context(tc.tile_pool(name="work", bufs=2))
        psum_t = stack.enter_context(tc.psum_pool(name="psum_t", bufs=3))
        psum_q = stack.enter_context(tc.psum_pool(name="psum_q", bufs=2))
        psum_s = stack.enter_context(tc.psum_pool(name="psum_s", bufs=1))
        psum_b = stack.enter_context(tc.psum_pool(name="psum_b", bufs=1))

        w_words = keep.tile([P, 2 * D], U8, align_bytes=64)
        w_plane = keep.tile([P, D], U8, align_bytes=64)
        ident = keep.tile([P, P], F32)
        ident_bf = keep.tile([P, P], BF16)
        bias_rows = keep.tile([P, P], BF16)
        bias_pairs = keep.tile([P, 2 * P], BF16)
        k_ext = keep.tile([P, ROWS, D], BF16)
        x_band = keep.tile([P, BAND_TILES, D], BF16)
        k_band = keep.tile([P, BAND_TILES, D], BF16)
        raw = keep.tile([P, RUN, SCORE_PAD], F32)
        slots = keep.tile([P, BAND_TILES, SLOTS], F32)
        flat_weights = keep.tile([P, 2 * P], F32, align_bytes=64)
        bias_dot = psum_b.tile([P, ROWS], F32)
        key_cols_0 = keep.tile([P, D_BLOCKS, SEQ + 2 * HALO], F32)
        key_cols_1 = keep.tile([P, D_BLOCKS, SEQ + 2 * HALO], F32)
        key_cols_2 = keep.tile([P, D_BLOCKS, SEQ + 2 * HALO], F32)
        key_cols = [key_cols_0, key_cols_1, key_cols_2]

        nc.vector.memset(w_plane[:].bitcast(I32), 0)
        nc.vector.memset(bias_rows[:], 0.0)
        nc.vector.memset(bias_pairs[:], 0.0)
        warm = keep.tile([P, 1], F32)
        nc.vector.memset(warm[:], 0.0)
        make_identity(nc, ident[:])
        nc.vector.tensor_copy(out=ident_bf[:], in_=ident[:])
        nc.scalar.activation(out=warm[:], in_=warm[:], func=ACT.Exp)
        for cols in key_cols:
            nc.vector.memset(cols[:, :, 0:HALO], 0.0)
            nc.vector.memset(cols[:, :, HALO + SEQ :], 0.0)

        diff_i = keep.tile([P, WINDOW], I32)
        nc.gpsimd.iota(diff_i[:], pattern=[[1, WINDOW]], base=0, channel_multiplier=-1)
        diff = keep.tile([P, WINDOW], F32)
        nc.vector.tensor_copy(out=diff[:], in_=diff_i[:])
        inside = keep.tile([P, WINDOW], F32)
        nc.vector.tensor_scalar(out=inside[:], in0=diff[:], scalar1=0.0, scalar2=None, op0=ALU.is_ge)
        nc.vector.scalar_tensor_tensor(
            out=inside[:], in0=diff[:], scalar=float(BAND - 1), in1=inside[:], op0=ALU.is_le, op1=ALU.mult
        )
        band_mask = keep.tile([P, SEQ_TILES, WINDOW], F32)
        for i in range(SEQ_TILES):
            nc.vector.tensor_scalar(
                out=band_mask[:, i, :], in0=inside[:], scalar1=1.0, scalar2=-MASKED, op0=ALU.subtract, op1=ALU.mult
            )
        nc.vector.memset(band_mask[:, 0, 0:HALO], MASKED)
        nc.vector.memset(band_mask[:, SEQ_TILES - 1, WINDOW - HALO :], MASKED)
        on_diag = keep.tile([P, WINDOW], F32)
        nc.vector.tensor_scalar(out=on_diag[:], in0=diff[:], scalar1=0.0, scalar2=None, op0=ALU.is_equal)
        turn = keep.tile([P, SLOTS], F32)
        nc.vector.tensor_reduce(
            out=turn[:], in_=on_diag[:].rearrange("p (a r) -> p r a", r=SLOTS), axis=AXIS_X, op=ALU.add
        )
        place_i = keep.tile([P, RUN], I32)
        nc.gpsimd.iota(place_i[:], pattern=[[1, RUN]], base=0, channel_multiplier=RUN)
        place_m = keep.tile([P, RUN], I32)
        nc.vector.tensor_scalar(out=place_m[:], in0=place_i[:], scalar1=SEQ - 1, scalar2=None, op0=ALU.bitwise_and)
        place = keep.tile([P, RUN], F32)
        nc.vector.tensor_copy(out=place[:], in_=place_m[:])
        edge = keep.tile([P, RUN, BAND], F32)
        nc.vector.memset(edge[:], 0.0)
        for j in range(HALO):
            nc.vector.tensor_scalar(
                out=edge[:, :, j], in0=place[:], scalar1=float(HALO - j), scalar2=MASKED, op0=ALU.is_lt, op1=ALU.mult
            )
            nc.vector.tensor_scalar(
                out=edge[:, :, BAND - 1 - j], in0=place[:], scalar1=float(SEQ - 1 - HALO + j), scalar2=MASKED,
                op0=ALU.is_gt, op1=ALU.mult,
            )

        nc.gpsimd.memset(k_ext[:, RUN + HALO :, :], 0.0)
        nc.gpsimd.memset(flat_weights[:], 0.0)

        def x_tick(first):
            return max(first - X_LEAD, first // 2 + FIRST_TICK - (1 if first == GROUP + PAIR else 0))

        def band_tick(s):
            return (s * BAND_NUM) // BAND_DEN

        def rows_tick(n):
            return 2 * n + 1 if n < ROWS_SINGLE else 2 * ROWS_SINGLE + (n - ROWS_SINGLE)

        def load_x_run(g):
            steps = slice(g * GROUP, (g + 1) * GROUP)
            x_groups[g] = x_pool.tile([P, GROUP, D], BF16, name="x_run")
            nc.sync.dma_start(out=x_groups[g][:], in_=x_steps[:, steps, :])

        def load_k_run(g):
            nc.sync.dma_start(
                out=k_ext[:, HALO + g * GROUP : HALO + (g + 1) * GROUP, :],
                in_=k_steps[:, g * GROUP : (g + 1) * GROUP, :],
            )

        def load_x_band(n):
            tiles = slice(2 * SEQ_TILES * n, 2 * SEQ_TILES * (n + 1))
            nc.sync.dma_start(out=x_band[:, tiles, :], in_=x_tiles[:, tiles, :])

        def load_k_band(n):
            tiles = slice(2 * SEQ_TILES * n, 2 * SEQ_TILES * (n + 1))
            nc.sync.dma_start(out=k_band[:, tiles, :], in_=k_tiles[:, tiles, :])

        x_first = x_pool.tile([P, GROUP, D], BF16, name="x_run")
        x_groups = {0: x_first}
        nc.sync.dma_start(out=x_first[:, 0:PAIR, :], in_=x_steps[:, 0:PAIR, :])
        nc.sync.dma_start(out=w_words[:].bitcast(I32), in_=Wq_words[0].bitcast(I32))
        nc.sync.dma_start(out=x_first[:, PAIR:GROUP, :], in_=x_steps[:, PAIR:GROUP, :])
        for quadrant in range(4):
            nc.sync.dma_start(
                out=w_plane[32 * quadrant : 32 * quadrant + 4, :].bitcast(I32),
                in_=Wq_scales[0, 4 * quadrant : 4 * quadrant + 4, :].bitcast(I32),
            )
        nc.scalar.dma_start(out=k_ext[:, 0:HALO, :], in_=k_before[:, 0:HALO, :])
        loads = []
        for g in range(1, X_GROUPS_HELD):
            loads.append((x_tick(g * GROUP), 0, load_x_run, g))
        for g in range(GROUPS):
            loads.append((g * GROUP - HALO - 1, 1, load_k_run, g))
        for n in range(BAND_SEQS // 2):
            loads.append((band_tick(2 * n), 2, load_x_band, n))
            loads.append((band_tick(2 * n) + 1, 3, load_k_band, n))
        def load_bias(n):
            nc.sync.dma_start(out=bias_rows[0:D_BLOCKS, :], in_=bq.rearrange("(c d) -> c d", c=D_BLOCKS))
            nc.sync.dma_start(out=bias_pairs[0:2, :], in_=bq.rearrange("(u n) -> u n", u=2))

        loads.append((x_tick(GROUP), 1, load_bias, 0))
        for entry in sorted(loads, key=lambda item: (item[0], item[1])):
            entry[2](entry[3])
        nc.sync.dma_start(out=k_ext[0:112, RUN + HALO :, :], in_=k_after[0:112, 0:HALO, :])
        nc.sync.dma_start(out=k_ext[112 : P - 1, RUN + HALO :, :], in_=k_after[112 : P - 1, 0:HALO, :])

        bias = {}

        def prepare_bias():
            bias_t = psum_t.tile([P, P], BF16, name="tp")
            nc.tensor.transpose(bias_t[:], bias_rows[:], ident_bf[:])
            bias_scaled = keep.tile([P, D_BLOCKS], F32)
            nc.scalar.activation(out=bias_scaled[:], in_=bias_t[:, 0:D_BLOCKS], func=ACT.Copy, scale=INV_SQRT_D)
            pair_t = psum_t.tile([P, P], F32, name="tp")
            nc.tensor.transpose(pair_t[:], bias_pairs[:].bitcast(F32), ident[:])
            bias_words = keep.tile([P, 2], F32)
            nc.scalar.copy(out=bias_words[:], in_=pair_t[:, 0:2])
            bias["scaled"] = bias_scaled
            bias["cols"] = bias_words[:].bitcast(BF16)

        def words_of(tile_ap, count):
            flat = tile_ap.rearrange("p t k -> p (t k)").bitcast(F32)
            return flat.rearrange("p (t w) -> p t w", t=count)

        x_band_words = words_of(x_band[:], BAND_TILES)
        k_words = words_of(k_ext[:], ROWS)

        def transpose_x_pair(words, first, dest, on_vector=False):
            xt = psum_t.tile([P, PAIR, 2, P], F32, name="tp")
            for i in range(PAIR):
                for u in range(2):
                    nc.tensor.transpose(xt[:, i, u, :], words[:, first + i, u : D // 2 : 2], ident[:])
            if on_vector:
                nc.vector.tensor_copy(out=dest, in_=xt[:].rearrange("q t u p -> q t p u"))
            else:
                nc.scalar.copy(out=dest, in_=xt[:].rearrange("q t u p -> q t p u"))

        grouped_of = {}
        quantised_of = {}

        def transpose_run_pair(first):
            g = first // GROUP
            if first % GROUP == 0:
                grouped_of[g] = quant.tile([P, GROUP * P * 4], BF16, align_bytes=64, name="grouped")
            grouped_words = grouped_of[g][:].bitcast(F32).rearrange("q (t p u) -> q t p u", t=GROUP, u=2)
            transpose_x_pair(words_of(x_groups[g][:], GROUP), first % GROUP, grouped_words[:, first % GROUP : first % GROUP + PAIR, :, :])

        def quantise_group(g):
            codes = quant.tile([P, GROUP * P], U32, align_bytes=64, name="codes")
            scales = quant.tile([P, GROUP * P], U8, align_bytes=64, name="scales")
            nc.vector.quantize_mx(out=codes[:].bitcast(FP8X4), scales=scales[:], in_=grouped_of[g][:])
            quantised_of[g] = (codes, scales)

        def quantise_first_pair(half):
            if half == 0:
                codes = quant.tile([P, GROUP * P], U32, align_bytes=64, name="codes")
                scales = quant.tile([P, GROUP * P], U8, align_bytes=64, name="scales")
                quantised_of[0] = (codes, scales)
            codes, scales = quantised_of[0]
            cols = slice(half * PAIR * P, (half + 1) * PAIR * P)
            nc.vector.quantize_mx(
                out=codes[:, cols].bitcast(FP8X4),
                scales=scales[:, cols],
                in_=grouped_of[0][:, half * PAIR * P * 4 : (half + 1) * PAIR * P * 4],
            )

        def project(t):
            codes, scales = quantised_of[t // GROUP]
            cols = slice((t % GROUP) * P, (t % GROUP + 1) * P)
            q_ps = psum_q.tile([P, D], F32, name="q_ps")
            nc.tensor.matmul_mx(
                out=q_ps[:],
                lhsT=codes[:, cols].bitcast(FP8X4),
                lhsT_scale=scales[:, cols],
                rhs=w_words[:].bitcast(FP4X4),
                rhs_scale=w_plane[:],
                start=True,
                stop=True,
            )
            return q_ps

        def scores_on_vector(t, q_ps, between):
            for j in range(BAND):
                for function in between.get(j, []):
                    function()
                junk = work.tile([P, D], BF16, name="junk", bufs=JUNK_BUFFERS)
                nc.vector.scalar_tensor_tensor(
                    out=junk[:],
                    in0=q_ps[:],
                    scalar=INV_SQRT_D,
                    in1=k_ext[:, t + j, :],
                    op0=ALU.mult,
                    op1=ALU.mult,
                    accum_out=raw[:, t, j : j + 1],
                )

        def copy_for_gpsimd(q_ps):
            q_sb = work.tile([P, D], F32, name="q_sb")
            nc.scalar.copy(out=q_sb[:], in_=q_ps[:])
            return q_sb

        def multiply_on_gpsimd(t, q_sb, gate):
            products = work.tile([P, BAND, D], F32, name="products")
            if gate:
                nc.vector.memset(products[:, 0, 0:1], 0.0)
            for low, high in ((0, 3), (3, BAND)):
                nc.gpsimd.tensor_tensor(
                    out=products[:, low:high, :],
                    in0=q_sb[:].unsqueeze(1).to_broadcast([P, high - low, D]),
                    in1=k_ext[:, t + low : t + high, :],
                    op=ALU.mult,
                )
            return products

        def sum_on_scalar(t, products, neighbours):
            for j in neighbours:
                nc.scalar.activation(
                    out=products[:, j, :],
                    in_=products[:, j, :],
                    func=ACT.Copy,
                    scale=INV_SQRT_D,
                    accum_out=raw[:, t, j : j + 1],
                )

        def transpose_rows(first):
            kw = psum_t.tile([P, PAIR, 2, P], F32, name="tp")
            for i in range(PAIR):
                for u in range(2):
                    nc.tensor.transpose(kw[:, i, u, :], k_words[:, first + i, u * P : (u + 1) * P], ident[:])
            kw_sb = rows_pool.tile([P, PAIR * 2 * P], F32, name="kw_sb")
            nc.scalar.copy(out=kw_sb[:], in_=kw[:].rearrange("w i u p -> w (i u p)"))
            return kw_sb

        def bias_dot_pair(first, kw_sb):
            halves = kw_sb[:].bitcast(BF16).rearrange("w (i u p e) -> w i u p e", i=PAIR, u=2, e=2)
            for i in range(PAIR):
                for n in range(4):
                    nc.tensor.matmul(
                        out=bias_dot[:, first + i : first + i + 1],
                        lhsT=halves[:, i, n // 2, :, n % 2],
                        rhs=bias["cols"][:, n : n + 1],
                        start=(n == 0),
                        stop=(n == 3),
                    )

        band_grouped = {}
        band_quantised = {}
        query_cols = {}
        band_scores_of = {}

        def band_x(s):
            grouped = quant.tile([P, SEQ * 4], BF16, align_bytes=64, name="grouped_b")
            dest = grouped[:].bitcast(F32).rearrange("q (t p u) -> q t p u", t=SEQ_TILES, u=2)
            transpose_x_pair(x_band_words, SEQ_TILES * s, dest, BAND_X_ON_VECTOR)
            band_grouped[s] = grouped

        def band_quantise(s):
            codes = quant.tile([P, SEQ], U32, align_bytes=64, name="codes_b")
            scales = quant.tile([P, SEQ], U8, align_bytes=64, name="scales_b")
            nc.vector.quantize_mx(out=codes[:].bitcast(FP8X4), scales=scales[:], in_=band_grouped[s][:])
            band_quantised[s] = (codes, scales)

        def band_k(s):
            kt = psum_t.tile([P, SEQ_TILES, D_BLOCKS, P], BF16, name="tp")
            for i in range(SEQ_TILES):
                for c in range(D_BLOCKS):
                    nc.tensor.transpose(kt[:, i, c, :], k_band[:, SEQ_TILES * s + i, c * P : (c + 1) * P], ident_bf[:])
            cols = key_cols[s % len(key_cols)]
            nc.scalar.copy(
                out=cols[:, :, HALO : HALO + SEQ].rearrange("d c (i n) -> d i c n", i=SEQ_TILES), in_=kt[:]
            )

        def band_q(s, half):
            codes, scales = band_quantised[s]
            if half == 0:
                query_cols[s] = work.tile([P, D_BLOCKS, SEQ], F32, name="q_cols")
            qt = psum_t.tile([P, 2, SEQ], F32, name="tp")
            for n in range(2):
                c = 2 * half + n
                nc.tensor.matmul_mx(
                    out=qt[:, n, :],
                    lhsT=w_words[:, 2 * P * c : 2 * P * (c + 1)].bitcast(FP4X4),
                    lhsT_scale=w_plane[:, P * c : P * (c + 1)],
                    rhs=codes[:].bitcast(FP8X4),
                    rhs_scale=scales[:],
                    start=True,
                    stop=True,
                )
            for n in range(2):
                c = 2 * half + n
                nc.scalar.activation(
                    out=query_cols[s][:, c, :],
                    in_=qt[:, n, :],
                    func=ACT.Identity,
                    bias=bias["scaled"][:, c : c + 1],
                    scale=INV_SQRT_D,
                )

        def band_q_first(s):
            band_q(s, 0)

        def band_q_second(s):
            band_q(s, 1)

        sc_0 = psum_s.tile([P, SEQ_TILES, WINDOW], F32)
        sc_1 = psum_s.tile([P, SEQ_TILES, WINDOW], F32)
        sc_of = [sc_0, sc_1]
        for scores in sc_of:
            nc.tensor.transpose(scores[:, 0, 0:P], ident[:], ident[:])
            nc.tensor.transpose(scores[:, 1, WINDOW - P : WINDOW], ident[:], ident[:])
        masked_of = {}

        def band_multiply(s, parts):
            cols = key_cols[s % len(key_cols)]
            for part in parts:
                i, c = divmod(part, D_BLOCKS)
                inside = slice(HALO if i == 0 else 0, WINDOW - HALO if i == SEQ_TILES - 1 else WINDOW)
                nc.tensor.matmul(
                    out=sc_of[s % 2][:, i, inside],
                    lhsT=query_cols[s][:, c, i * P : (i + 1) * P],
                    rhs=cols[:, c, i * P + inside.start : i * P + inside.stop],
                    start=(c == 0),
                    stop=(c == D_BLOCKS - 1),
                )

        def band_mask_scores(s):
            masked_of[s] = work.tile([P, SEQ_TILES, WINDOW], F32, name="masked")
            nc.vector.tensor_tensor(out=masked_of[s][:], in0=sc_of[s % 2][:], in1=band_mask[:], op=ALU.add)

        def band_pick(s):
            nc.vector.tensor_reduce(
                out=slots[:, SEQ_TILES * s : SEQ_TILES * (s + 1), :],
                in_=masked_of[s][:].rearrange("p i (a r) -> p i r a", r=SLOTS),
                axis=AXIS_X,
                op=ALU.max,
            )

        def softmax_steps(label, scores, weights, dest, count, by_token, over_neighbours):
            top = keep.tile([P, count], F32, name="top_" + label)
            total = keep.tile([P, count], F32, name="total_" + label)
            return [
                lambda: nc.vector.tensor_reduce(out=top[:], in_=by_token(scores), axis=AXIS_X, op=ALU.max),
                lambda: nc.vector.tensor_tensor(out=weights, in0=scores, in1=over_neighbours(top[:]), op=ALU.subtract),
                lambda: nc.scalar.activation(out=weights, in_=weights, func=ACT.Exp),
                lambda: nc.vector.tensor_reduce(out=total[:], in_=by_token(weights), axis=AXIS_X, op=ALU.add),
                lambda: nc.vector.reciprocal(out=total[:], in_=total[:]),
                lambda: nc.vector.tensor_tensor(out=dest, in0=weights, in1=over_neighbours(total[:]), op=ALU.mult),
            ]

        twice = keep.tile([P, BAND_TILES, 2, SLOTS], F32)
        turned = keep.tile([P, SLOTS, BAND, BAND_TILES], F32)
        band_sc = keep.tile([P, BAND, BAND_TILES], F32)

        def turn_slots():
            nc.scalar.copy(out=twice[:], in_=slots[:].unsqueeze(2).to_broadcast([P, BAND_TILES, 2, SLOTS]))
            wrapped = twice[:].rearrange("p i w r -> p i (w r)")
            for r in range(SLOTS):
                nc.scalar.activation(
                    out=turned[:, r, :, :],
                    in_=wrapped[:, :, r : r + BAND].rearrange("p i j -> p j i"),
                    func=ACT.Copy,
                    scale=turn[:, r : r + 1],
                )

        def add_turned():
            nc.vector.tensor_reduce(
                out=band_sc[:], in_=turned[:].rearrange("p r j i -> p j i r"), axis=AXIS_X, op=ALU.add
            )

        band_weights = keep.tile([P, BAND, BAND_TILES], F32)
        flat_turned = keep.tile([P, 2 * P], F32, align_bytes=64)
        band_out = keep.tile([P, QUADRANT, BAND], F32)

        def store_band():
            for a in range(QUADRANTS):
                queue = nc.sync if a % 2 == 0 else nc.scalar
                queue.dma_start(
                    out=out_band[a],
                    in_=band_out[QUADRANT * a : QUADRANT * a + BAND_TILES, :, :].rearrange("t p j -> t (p j)"),
                )

        band_steps = softmax_steps(
            "band",
            band_sc[:],
            band_weights[:],
            flat_weights[:, 0 : BAND * QUADRANT].rearrange("p (j t) -> p j t", j=BAND)[:, :, 0:BAND_TILES],
            BAND_TILES,
            lambda view: view.rearrange("p j i -> p i j"),
            lambda stat: stat.unsqueeze(1).to_broadcast([P, BAND, BAND_TILES]),
        )
        band_steps += [
            lambda: nc.vector.transpose(out=flat_turned[:], in_=flat_weights[:]),
            lambda: nc.scalar.copy(
                out=band_out[:], in_=flat_turned[:, 0 : BAND * QUADRANT].rearrange("q (j p) -> q p j", j=BAND)
            ),
            store_band,
        ]

        def is_gpsimd_tick(tick):
            return 0 <= tick < RUN and tick % GPSIMD_EVERY == 1

        def next_gpsimd_tick(tick):
            while not is_gpsimd_tick(tick):
                tick += 1
            return tick

        products_of = {}
        q_of = {}
        project_at = {}
        for t in range(RUN):
            project_at.setdefault(t - 1 if 0 < t <= 1 else t, []).append(t)
        rows_of = {}
        addend = keep.tile([P, RUN, BAND], F32)
        x_at = {}
        quant_at = {}
        rows_at = {}
        band_at = {}
        for first in range(0, RUN, PAIR):
            x_at.setdefault(x_tick(first), []).append(first)
        def last_gpsimd_tick(tick):
            while not is_gpsimd_tick(tick):
                tick -= 1
            return tick
        for g in range(1, GROUPS):
            quant_at.setdefault(last_gpsimd_tick(g * GROUP - 1), []).append(g)
        for n in range(ROWS // PAIR):
            rows_at[rows_tick(n)] = PAIR * n
        project_tick = 0
        for s in range(BAND_SEQS):
            quantise_tick = next_gpsimd_tick(band_tick(s) + 1)
            project_tick = max(quantise_tick + 1, project_tick + 2)
            band_at.setdefault(band_tick(s), []).append(("x", s))
            band_at.setdefault(quantise_tick, []).append(("quantise", s))
            band_at.setdefault(project_tick - 1, []).append(("k", s))
            for depth in range(6):
                band_at.setdefault(project_tick + depth, []).append((depth, s))

        for tick in range(FIRST_TICK, LAST_TICK):
            in_run = 0 <= tick < RUN
            on_gpsimd = is_gpsimd_tick(tick)
            band_now = band_at.get(tick, [])
            q_ps = None
            q_sb = None
            for t in project_at.get(tick, []):
                q_of[t] = project(t)
            if in_run:
                q_ps = q_of[tick]
            if on_gpsimd:
                q_sb = copy_for_gpsimd(q_ps)
            for what, s in band_now:
                if what == 4:
                    band_multiply(s, (6, 7))
            for what, s in band_now:
                if what == 0:
                    band_q(s, 0)
                if what == 1:
                    band_q(s, 1)
            for lag, neighbours in SUM_PLAN:
                if tick - lag in products_of:
                    sum_on_scalar(tick - lag, products_of[tick - lag], neighbours)
            if tick - 2 in rows_of:
                bias_dot_pair(*rows_of[tick - 2])
            if tick == 0:
                prepare_bias()
            for what, s in band_now:
                if what == 2:
                    band_multiply(s, (0, 1))
                if what == 3:
                    band_multiply(s, (3, 4))
            for first in x_at.get(tick, []):
                transpose_run_pair(first)
                g = first // GROUP + X_GROUPS_HELD
                if first % GROUP == GROUP - PAIR and g < GROUPS:
                    load_x_run(g)
            if tick in rows_at:
                rows_of[tick] = (rows_at[tick], transpose_rows(rows_at[tick]))
            for what, s in band_now:
                if what == "x":
                    band_x(s)
            for what, s in band_now:
                if what == "k":
                    band_k(s)
            for what, s in band_now:
                if what == 2:
                    band_multiply(s, (2,))
                if what == 3:
                    band_multiply(s, (5,))
            picks = []
            between = {}
            for what, s in band_now:
                if what == 5:
                    band_mask_scores(s)
                    picks.append(lambda s=s: band_pick(s))
            gate = False
            if tick < 0:
                quantise_first_pair(tick - FIRST_TICK)
            for g in quant_at.get(tick, []):
                quantise_group(g)
                gate = True
            for what, s in band_now:
                if what == "quantise":
                    band_quantise(s)
                    gate = True
            if on_gpsimd:
                products_of[tick] = multiply_on_gpsimd(tick, q_sb, gate)
            if tick == RUN - 1:
                for j in range(BAND):
                    nc.vector.scalar_tensor_tensor(
                        out=addend[:, :, j],
                        in0=bias_dot[:, j : j + RUN],
                        scalar=INV_SQRT_D,
                        in1=edge[:, :, j],
                        op0=ALU.mult,
                        op1=ALU.add,
                    )
            if tick == RUN - 1:
                picks.append(add_turned)
                between = {2: [band_steps[0]], 4: [band_steps[1]]}
            if in_run and not on_gpsimd:
                scores_on_vector(tick, q_ps, dict([(1, picks)] + list(between.items())))
            else:
                for pick in picks:
                    pick()
            if tick == TURN_TICK:
                turn_slots()

        scores = keep.tile([P, RUN, BAND], F32)
        run_weights = keep.tile([P, RUN, BAND], F32)
        run_steps = [
            lambda: nc.vector.tensor_tensor(out=scores[:], in0=raw[:, :, 0:BAND], in1=addend[:], op=ALU.add)
        ]
        run_steps += softmax_steps(
            "run", scores[:], run_weights[:], run_weights[:], RUN,
            lambda view: view,
            lambda stat: stat.unsqueeze(2).to_broadcast([P, RUN, BAND]),
        )
        run_steps += [lambda: nc.sync.dma_start(out=out_run, in_=run_weights[:].rearrange("p t j -> p (t j)"))]
        band_steps[2]()
        for step, run_step in enumerate(run_steps):
            run_step()
            if step + 3 < len(band_steps):
                band_steps[step + 3]()
